import numpy as np
import ml_dtypes


def mxq(x, axis, fmt="e4m3"):
    dtype, down = {"e4m3": (ml_dtypes.float8_e4m3fn, 7), "e5m2": (ml_dtypes.float8_e5m2, 14)}[fmt]
    v = np.moveaxis(np.asarray(x, np.float32).astype(ml_dtypes.bfloat16).astype(np.float64), axis, -1)
    blocks = v.reshape(v.shape[:-1] + (-1, 32))
    amax = np.abs(blocks).max(-1, keepdims=True)
    byte = np.maximum(np.where(amax > 0, np.frexp(amax)[1] - 1 + 127, 0) - down, 1)
    scale = np.exp2(byte - 127.0)
    codes = (blocks / scale).astype(np.float32).astype(dtype).astype(np.float64)
    return np.moveaxis((codes * scale).reshape(v.shape), -1, axis)


WIDE = False


def mx_kscale(k):
    if not WIDE:
        return np.ones(k)
    levels = np.array([10, -10, 5, -5, 0])
    a = np.random.permutation(np.resize(levels, k // 512 * 4)).reshape(k // 512, 4)
    idx = np.arange(k)
    return np.exp2(a[idx // 512, idx % 128 // 32])


BF16 = ml_dtypes.bfloat16


def bf(x):
    return np.asarray(x, np.float32).astype(BF16)


def f64(x):
    return np.asarray(x).astype(np.float64)


E2M1 = np.array([0.0, 0.5, 1.0, 1.5, 2.0, 3.0, 4.0, 6.0, -0.0, -0.5, -1.0, -1.5, -2.0, -3.0, -4.0, -6.0])


def pack_weight(w, fmt):
    k, n = w.shape
    w = f64(bf(w)).reshape(k // 32, 32, n)
    amax = np.abs(w).max(1)
    if fmt == "e4m3":
        byte = np.frexp(amax)[1] - 1 + 127 - 7
    else:
        mant, ex = np.frexp(amax / 6.0)
        byte = np.where(mant > 0.5, ex, ex - 1) + 127
    byte = np.clip(np.where(amax > 0, byte, 1), 1, 254)
    scaled = (w * np.exp2(127.0 - byte)[:, None, :]).reshape(k, n).astype(np.float32)
    by_word = np.ascontiguousarray(scaled.reshape(k // 512, 128, 4, n).transpose(0, 1, 3, 2))
    if fmt == "e4m3":
        words = by_word.astype(ml_dtypes.float8_e4m3fn).view(np.uint8)
    else:
        c = by_word.astype(ml_dtypes.float4_e2m1fn).view(np.uint8) & 0xF
        words = c[..., 0::2] | (c[..., 1::2] << 4)
    return np.ascontiguousarray(words), np.ascontiguousarray(byte.astype(np.uint8).reshape(k // 512, 16, n))


def unpack_weight(words, scales, fmt):
    g, p, n, _ = words.shape
    if fmt == "e4m3":
        vals = np.ascontiguousarray(words).view(ml_dtypes.float8_e4m3fn).astype(np.float64)
    else:
        nib = np.empty((g, p, n, 4), np.uint8)
        nib[..., 0::2] = words & 0xF
        nib[..., 1::2] = words >> 4
        vals = E2M1[nib]
    vals = vals * np.repeat(np.exp2(scales.astype(np.float64) - 127.0), 8, axis=1)[..., None]
    return vals.transpose(0, 1, 3, 2).reshape(g * 512, n)


B, H = 128, 2048
EPS = 1e-5
FMT = "e4m3"


def layernorm(x, gamma, beta):
    mu = np.mean(x, axis=-1, keepdims=True)
    var = np.var(x, axis=-1, keepdims=True)
    return (x - mu) / np.sqrt(var + EPS) * gamma + beta


def sigmoid(v):
    return 1.0 / (1.0 + np.exp(-v))


def setup_inputs():
    s = mx_kscale(H)
    inp = bf(np.random.standard_normal((B, H)) * s)
    hx = bf(np.random.standard_normal((B, H)))
    W_words, W_scales = pack_weight(np.random.standard_normal((H, 3 * H)) / np.sqrt(H) / s[:, None], FMT)
    U_words, U_scales = pack_weight(np.random.standard_normal((H, 3 * H)) / np.sqrt(H), FMT)
    return {"input": inp,
            "hx": hx,
            "W_words": W_words,
            "W_scales": W_scales,
            "U_words": U_words,
            "U_scales": U_scales,
            "b": bf(np.random.standard_normal(3 * H) * 0.1),
            "W_gamma": bf(1.0 + np.random.standard_normal(3 * H) * 0.1),
            "W_beta": bf(np.random.standard_normal(3 * H) * 0.1),
            "U_gamma": bf(1.0 + np.random.standard_normal(3 * H) * 0.1),
            "U_beta": bf(np.random.standard_normal(3 * H) * 0.1)}


def reference(input, hx, W_words, W_scales, U_words, U_scales, b, W_gamma, W_beta, U_gamma, U_beta):
    hx = f64(hx)
    b = f64(b)
    xw = layernorm(mxq(f64(input), 1, "e4m3") @ unpack_weight(W_words, W_scales, FMT), f64(W_gamma), f64(W_beta))
    hu = layernorm(mxq(hx, 1, "e4m3") @ unpack_weight(U_words, U_scales, FMT), f64(U_gamma), f64(U_beta))
    xw0, xw1, xw2 = xw[:, :H], xw[:, H:2 * H], xw[:, 2 * H:]
    hu0, hu1, hu2 = hu[:, :H], hu[:, H:2 * H], hu[:, 2 * H:]
    b0, b1, b2 = b[:H], b[H:2 * H], b[2 * H:]
    z = sigmoid(xw0 + hu0 + b0)
    r = sigmoid(xw1 + hu1 + b1)
    hx_ = np.tanh(r * hu2 + xw2 + b2)
    return (1.0 - z) * hx_ + z * hx

@@ -1,0 +1,248 @@
+from contextlib import ExitStack
+
+import concourse.mybir as mybir
+from concourse.masks import make_identity
+
+F32 = mybir.dt.float32
+BF16 = mybir.dt.bfloat16
+I32 = mybir.dt.int32
+U8 = mybir.dt.uint8
+FP8X4 = mybir.dt.float8_e4m3fn_x4
+ALU = mybir.AluOpType
+ACT = mybir.ActivationFunctionType
+
+P = 128
+H = 2048
+N3 = 3 * H
+KG = 4
+NB = 512
+EPS = 1e-5
+FLOPS = 2 * 2 * P * H * N3
+
+
+def tile_lngrucell_w_kernel(
+    tc, x_in, hx, W_words, W_scales, U_words, U_scales, b, W_gamma, W_beta, U_gamma, U_beta, out
+):
+    nc = tc.nc
+    with ExitStack() as ctx:
+        keep = ctx.enter_context(tc.tile_pool(name="keep", bufs=1))
+        wpool = ctx.enter_context(tc.tile_pool(name="wpool", bufs=10))
+        psmx = ctx.enter_context(tc.psum_pool(name="psmx", bufs=2))
+        psaux = ctx.enter_context(tc.psum_pool(name="psaux", bufs=6))
+
+        planes_w = keep.tile([P, N3], U8, name="planes_w", align_bytes=64)
+        planes_u = keep.tile([P, N3], U8, name="planes_u", align_bytes=64)
+        x_sb = keep.tile([P, H], BF16, name="x_sb", align_bytes=64)
+        h_sb = keep.tile([P, H], BF16, name="h_sb", align_bytes=64)
+        grp_x = keep.tile([P, H], BF16, name="grp_x", align_bytes=64)
+        grp_h = keep.tile([P, H], BF16, name="grp_h", align_bytes=64)
+        cod_x = keep.tile([P, H // 4], I32, name="cod_x", align_bytes=64)
+        cod_h = keep.tile([P, H // 4], I32, name="cod_h", align_bytes=64)
+        pln_x = keep.tile([P, H // 4], U8, name="pln_x", align_bytes=64)
+        pln_h = keep.tile([P, H // 4], U8, name="pln_h", align_bytes=64)
+        ident_f = keep.tile([P, P], F32, name="ident_f")
+        ident_b = keep.tile([P, P], BF16, name="ident_b")
+        vecrows = keep.tile([P, P], BF16, name="vecrows")
+        g_t = keep.tile([P, P], BF16, name="g_t")
+        g_w = keep.tile([P, N3], BF16, name="g_w")
+        g_u = keep.tile([P, N3], BF16, name="g_u")
+        rk = keep.tile([P, N3], BF16, name="rk")
+        p_w = keep.tile([P, N3], F32, name="p_w")
+        p_u = keep.tile([P, N3], F32, name="p_u")
+        st_w = keep.tile([P, 12, 6], F32, name="st_w")
+        st_u = keep.tile([P, 12, 6], F32, name="st_u")
+        csp_w = keep.tile([P, P], BF16, name="csp_w")
+        csp_u = keep.tile([P, P], BF16, name="csp_u")
+        neghalf = keep.tile([P, 1], F32, name="neghalf")
+        warm_in = keep.tile([P, 1], F32, name="warm_in")
+        warm_out = keep.tile([P, 1], F32, name="warm_out")
+
+        nc.vector.memset(planes_w[:].bitcast(I32), 0)
+        nc.vector.memset(planes_u[:].bitcast(I32), 0)
+        nc.vector.memset(warm_in[:], 0.0)
+        nc.vector.memset(neghalf[:], -0.5)
+        nc.vector.memset(csp_w[:], 0.0)
+        nc.vector.memset(csp_u[:], 0.0)
+        nc.vector.memset(csp_w[:, 6:9], 1.0)
+        nc.vector.memset(csp_u[:, 9:10], 1.0)
+
+        nc.sync.dma_start(out=x_sb[:], in_=x_in)
+        for planes, scales in ((planes_w, W_scales), (planes_u, U_scales)):
+            s32 = scales.bitcast(I32)
+            for q in range(4):
+                nc.sync.dma_start(
+                    out=planes[32 * q : 32 * q + 16, :].bitcast(I32),
+                    in_=s32[:, 4 * q : 4 * q + 4, :],
+                )
+        nc.sync.dma_start(out=h_sb[:], in_=hx)
+
+        nc.scalar.dma_start(out=vecrows[0:48, :], in_=W_gamma.rearrange("(j p) -> j p", p=P))
+        nc.scalar.dma_start(out=vecrows[48:96, :], in_=U_gamma.rearrange("(j p) -> j p", p=P))
+        nc.scalar.dma_start(out=vecrows[96:128, :], in_=W_beta[0:4096].rearrange("(j p) -> j p", p=P))
+        nc.scalar.activation(out=warm_out[:], in_=warm_in[:], func=ACT.Sigmoid)
+
+        make_identity(nc, ident_f[:])
+        make_identity(nc, ident_b[:])
+        nc.gpsimd.memset(rk[:].bitcast(F32), 0.0)
+        nc.gpsimd.dma_start(out=rk[0:3, :], in_=W_gamma.partition_broadcast(3))
+        nc.gpsimd.dma_start(out=rk[3:6, :], in_=U_gamma.partition_broadcast(3))
+        nc.gpsimd.dma_start(out=rk[6:7, :], in_=W_beta.partition_broadcast(1))
+        nc.gpsimd.dma_start(out=rk[7:8, :], in_=b.partition_broadcast(1))
+        nc.gpsimd.dma_start(out=rk[8:9, 0 : 2 * H], in_=U_beta[0 : 2 * H].partition_broadcast(1))
+        nc.gpsimd.dma_start(out=rk[9:10, 2 * H : N3], in_=U_beta[2 * H : N3].partition_broadcast(1))
+
+        def regroup(src, grp):
+            words = src[:].bitcast(F32)
+            gview = grp[:].bitcast(F32).rearrange("p (g r u) -> p g r u", g=KG, r=P, u=2)
+            for half in range(2):
+                xt = psaux.tile([P, 4, P], F32, name="xt", tag="aux")
+                for gg in range(2):
+                    g = 2 * half + gg
+                    for u in range(2):
+                        nc.tensor.transpose(
+                            out=xt[:, 2 * gg + u, :],
+                            in_=words[:, 256 * g + u : 256 * (g + 1) : 2],
+                            identity=ident_f[:],
+                        )
+                nc.vector.tensor_copy(
+                    out=gview[:, 2 * half : 2 * half + 2, :, :],
+                    in_=xt[:].rearrange("p (g u) r -> p g r u", g=2, u=2),
+                )
+
+        regroup(x_sb, grp_x)
+        regroup(h_sb, grp_h)
+        nc.vector.quantize_mx(out=cod_x[:].bitcast(FP8X4), scales=pln_x[:], in_=grp_x[:])
+        nc.vector.quantize_mx(out=cod_h[:].bitcast(FP8X4), scales=pln_h[:], in_=grp_h[:])
+
+        gt_ps = psaux.tile([P, P], BF16, name="gt_ps", tag="aux")
+        nc.tensor.transpose(out=gt_ps[:], in_=vecrows[:], identity=ident_b[:])
+        nc.scalar.copy(out=g_t[:], in_=gt_ps[:])
+
+        def spread(dst, first):
+            for blk in range(6):
+                pg = psaux.tile([P, 1024], BF16, name="pg", tag="aux")
+                for i in range(8):
+                    j = first + 8 * blk + i
+                    nc.tensor.transpose(
+                        out=pg[:, P * i : P * (i + 1)],
+                        in_=g_t[:, j : j + 1].to_broadcast([P, P]),
+                        identity=ident_b[:],
+                    )
+                nc.scalar.copy(out=dst[:, 1024 * blk : 1024 * (blk + 1)], in_=pg[:])
+
+        spread(g_w, 0)
+        spread(g_u, 48)
+
+        def project(words, planes, cod, pln, gam, prod, stats, blocks):
+            w32 = words.rearrange("g p n t -> p g (n t)").bitcast(I32)
+            bank = 0
+            for c0, width in blocks:
+                per = H // width
+                tiles = []
+                for t in range(KG // per):
+                    wt = wpool.tile([P, H], I32, name="wt", tag="wt", align_bytes=64)
+                    nc.sync.dma_start(
+                        out=wt[:].rearrange("p (g n) -> p g n", g=per),
+                        in_=w32[:, t * per : (t + 1) * per, c0 : c0 + width],
+                    )
+                    tiles.append(wt)
+                for jj in range(width // NB):
+                    n0 = c0 + NB * jj
+                    acc = psmx.tile([P, NB], F32, name="acc", tag="acc")
+                    for g in range(KG):
+                        lo = (g % per) * width + NB * jj
+                        nc.tensor.matmul_mx(
+                            out=acc[:],
+                            lhsT=cod[:, P * g : P * (g + 1)].bitcast(FP8X4),
+                            lhsT_scale=pln[:, P * g : P * (g + 1)],
+                            rhs=tiles[g // per][:, lo : lo + NB].bitcast(FP8X4),
+                            rhs_scale=planes[4 * g : P, n0 : n0 + NB],
+                            start=(g == 0),
+                            stop=(g == KG - 1),
+                        )
+                    nc.vector.bn_stats(out=stats[:, bank, :], in_=acc[:])
+                    nc.vector.tensor_tensor(
+                        out=prod[:, n0 : n0 + NB], in0=acc[:], in1=gam[:, n0 : n0 + NB], op=ALU.mult
+                    )
+                    bank += 1
+
+        def ln_scalars(stats, csp, col, tagname):
+            mv = keep.tile([P, 2], F32, name="mv_" + tagname)
+            ve = keep.tile([P, 1], F32, name="ve_" + tagname)
+            rstd = keep.tile([P, 1], F32, name="rstd_" + tagname)
+            shift = keep.tile([P, 1], F32, name="shift_" + tagname)
+            rest = keep.tile([P, 1], F32, name="rest_" + tagname)
+            lhs = keep.tile([P, P], BF16, name="lhs_" + tagname)
+            nc.vector.bn_aggr(out=mv[:], in_=stats[:].rearrange("p j s -> p (j s)"))
+            nc.vector.tensor_scalar_add(out=ve[:], in0=mv[:, 1:2], scalar1=EPS)
+            nc.gpsimd.tensor_tensor(out=rstd[:], in0=ve[:], in1=neghalf[:], op=ALU.pow)
+            nc.vector.tensor_scalar(
+                out=shift[:], in0=mv[:, 0:1], scalar1=rstd[:, 0:1], scalar2=-1.0, op0=ALU.mult, op1=ALU.mult
+            )
+            nc.vector.tensor_copy(out=csp[:, col : col + 1], in_=shift[:])
+            nc.vector.tensor_tensor(out=rest[:], in0=shift[:], in1=csp[:, col : col + 1], op=ALU.subtract)
+            nc.vector.tensor_copy(out=csp[:, col + 1 : col + 2], in_=rest[:])
+            nc.vector.tensor_tensor(
+                out=csp[:, col + 2 : col + 3], in0=rest[:], in1=csp[:, col + 1 : col + 2], op=ALU.subtract
+            )
+            ct = psaux.tile([P, P], BF16, name="ct", tag="aux")
+            nc.tensor.transpose(out=ct[:], in_=csp[:], identity=ident_b[:])
+            nc.vector.tensor_copy(out=lhs[:], in_=ct[:])
+            return rstd, lhs
+
+        def rank_terms(lhs, n0):
+            r_ps = psaux.tile([P, NB], F32, name="r_ps", tag="aux")
+            nc.tensor.matmul(out=r_ps[:], lhsT=lhs[:], rhs=rk[:, n0 : n0 + NB], start=True, stop=True)
+            return r_ps
+
+        project(W_words, planes_w, cod_x, pln_x, g_w, p_w, st_w, [(0, H), (H, H), (2 * H, H)])
+        rstd_w, lhs_w = ln_scalars(st_w, csp_w, 0, "w")
+        for j in range(12):
+            n0 = NB * j
+            r_ps = rank_terms(lhs_w, n0)
+            nc.vector.scalar_tensor_tensor(
+                out=p_w[:, n0 : n0 + NB], in0=p_w[:, n0 : n0 + NB], scalar=rstd_w[:, 0:1], in1=r_ps[:],
+                op0=ALU.mult, op1=ALU.add,
+            )
+
+        project(
+            U_words, planes_u, cod_h, pln_h, g_u, p_u, st_u,
+            [(H, H), (2 * H, H), (0, 1024), (1024, NB), (1536, NB)],
+        )
+        rstd_u, lhs_u = ln_scalars(st_u, csp_u, 3, "u")
+
+        for j in range(4):
+            c1 = slice(H + NB * j, H + NB * (j + 1))
+            nc.vector.scalar_tensor_tensor(
+                out=p_u[:, c1], in0=p_u[:, c1], scalar=rstd_u[:, 0:1], in1=p_w[:, c1], op0=ALU.mult, op1=ALU.add
+            )
+        for j in range(4):
+            c1 = slice(H + NB * j, H + NB * (j + 1))
+            r_ps = rank_terms(lhs_u, H + NB * j)
+            nc.vector.tensor_tensor(out=p_u[:, c1], in0=p_u[:, c1], in1=r_ps[:], op=ALU.add)
+            nc.scalar.activation(out=p_u[:, c1], in_=p_u[:, c1], func=ACT.Sigmoid)
+        for j in range(4):
+            c1 = slice(H + NB * j, H + NB * (j + 1))
+            c2 = slice(2 * H + NB * j, 2 * H + NB * (j + 1))
+            r_ps = rank_terms(lhs_u, 2 * H + NB * j)
+            nc.vector.scalar_tensor_tensor(
+                out=p_u[:, c2], in0=p_u[:, c2], scalar=rstd_u[:, 0:1], in1=r_ps[:], op0=ALU.mult, op1=ALU.add
+            )
+            nc.vector.tensor_tensor(out=p_u[:, c2], in0=p_u[:, c2], in1=p_u[:, c1], op=ALU.mult)
+            nc.vector.tensor_tensor(out=p_u[:, c2], in0=p_u[:, c2], in1=p_w[:, c2], op=ALU.add)
+            nc.scalar.activation(out=p_u[:, c2], in_=p_u[:, c2], func=ACT.Tanh)
+        for j in range(4):
+            c0 = slice(NB * j, NB * (j + 1))
+            r_ps = rank_terms(lhs_u, NB * j)
+            nc.vector.scalar_tensor_tensor(
+                out=p_u[:, c0], in0=p_u[:, c0], scalar=rstd_u[:, 0:1], in1=p_w[:, c0], op0=ALU.mult, op1=ALU.add
+            )
+            nc.vector.tensor_tensor(out=p_u[:, c0], in0=p_u[:, c0], in1=r_ps[:], op=ALU.add)
+            nc.scalar.activation(out=p_u[:, c0], in_=p_u[:, c0], func=ACT.Sigmoid)
+        for j in range(4):
+            c0 = slice(NB * j, NB * (j + 1))
+            c2 = slice(2 * H + NB * j, 2 * H + NB * (j + 1))
+            nc.vector.tensor_tensor(out=p_w[:, c0], in0=h_sb[:, c0], in1=p_u[:, c2], op=ALU.subtract)
+            nc.vector.tensor_tensor(out=p_w[:, c0], in0=p_w[:, c0], in1=p_u[:, c0], op=ALU.mult)
+            nc.vector.tensor_tensor(out=p_w[:, c0], in0=p_w[:, c0], in1=p_u[:, c2], op=ALU.add)
+            nc.sync.dma_start(out=out[:, c0], in_=p_w[:, c0])

@@ -26,9 +26,11 @@ def tile_lngrucell_w_kernel(
     nc = tc.nc
     with ExitStack() as ctx:
         keep = ctx.enter_context(tc.tile_pool(name="keep", bufs=1))
-        wpool = ctx.enter_context(tc.tile_pool(name="wpool", bufs=10))
-        psmx = ctx.enter_context(tc.psum_pool(name="psmx", bufs=2))
-        psaux = ctx.enter_context(tc.psum_pool(name="psaux", bufs=6))
+        wpool = ctx.enter_context(tc.tile_pool(name="wpool", bufs=12))
+        psum = ctx.enter_context(tc.psum_pool(name="psum", bufs=1))
+
+        def bank(i, shape, dtype):
+            return psum.tile(shape, dtype, name="ps%d" % i, tag="b%d" % i)
 
         planes_w = keep.tile([P, N3], U8, name="planes_w", align_bytes=64)
         planes_u = keep.tile([P, N3], U8, name="planes_u", align_bytes=64)
@@ -46,13 +48,12 @@ def tile_lngrucell_w_kernel(
         g_t = keep.tile([P, P], BF16, name="g_t")
         g_w = keep.tile([P, N3], BF16, name="g_w")
         g_u = keep.tile([P, N3], BF16, name="g_u")
-        rk = keep.tile([P, N3], BF16, name="rk")
+        rk = keep.tile([P, 4 * H], BF16, name="rk")
         p_w = keep.tile([P, N3], F32, name="p_w")
         p_u = keep.tile([P, N3], F32, name="p_u")
         st_w = keep.tile([P, 12, 6], F32, name="st_w")
         st_u = keep.tile([P, 12, 6], F32, name="st_u")
-        csp_w = keep.tile([P, P], BF16, name="csp_w")
-        csp_u = keep.tile([P, P], BF16, name="csp_u")
+        csp = keep.tile([P, P], BF16, name="csp")
         neghalf = keep.tile([P, 1], F32, name="neghalf")
         warm_in = keep.tile([P, 1], F32, name="warm_in")
         warm_out = keep.tile([P, 1], F32, name="warm_out")
@@ -61,12 +62,11 @@ def tile_lngrucell_w_kernel(
         nc.vector.memset(planes_u[:].bitcast(I32), 0)
         nc.vector.memset(warm_in[:], 0.0)
         nc.vector.memset(neghalf[:], -0.5)
-        nc.vector.memset(csp_w[:], 0.0)
-        nc.vector.memset(csp_u[:], 0.0)
-        nc.vector.memset(csp_w[:, 6:9], 1.0)
-        nc.vector.memset(csp_u[:, 9:10], 1.0)
+        nc.vector.memset(csp[:], 0.0)
+        nc.vector.memset(csp[:, 6:10], 1.0)
 
         nc.sync.dma_start(out=x_sb[:], in_=x_in)
+        nc.sync.dma_start(out=h_sb[:], in_=hx)
         for planes, scales in ((planes_w, W_scales), (planes_u, U_scales)):
             s32 = scales.bitcast(I32)
             for q in range(4):
@@ -74,7 +74,6 @@ def tile_lngrucell_w_kernel(
                     out=planes[32 * q : 32 * q + 16, :].bitcast(I32),
                     in_=s32[:, 4 * q : 4 * q + 4, :],
                 )
-        nc.sync.dma_start(out=h_sb[:], in_=hx)
 
         nc.scalar.dma_start(out=vecrows[0:48, :], in_=W_gamma.rearrange("(j p) -> j p", p=P))
         nc.scalar.dma_start(out=vecrows[48:96, :], in_=U_gamma.rearrange("(j p) -> j p", p=P))
@@ -84,18 +83,21 @@ def tile_lngrucell_w_kernel(
         make_identity(nc, ident_f[:])
         make_identity(nc, ident_b[:])
         nc.gpsimd.memset(rk[:].bitcast(F32), 0.0)
-        nc.gpsimd.dma_start(out=rk[0:3, :], in_=W_gamma.partition_broadcast(3))
-        nc.gpsimd.dma_start(out=rk[3:6, :], in_=U_gamma.partition_broadcast(3))
-        nc.gpsimd.dma_start(out=rk[6:7, :], in_=W_beta.partition_broadcast(1))
-        nc.gpsimd.dma_start(out=rk[7:8, :], in_=b.partition_broadcast(1))
+        nc.gpsimd.dma_start(out=rk[0:3, 0 : 2 * H], in_=W_gamma[0 : 2 * H].partition_broadcast(3))
+        nc.gpsimd.dma_start(out=rk[0:3, 3 * H : 4 * H], in_=W_gamma[2 * H : N3].partition_broadcast(3))
+        nc.gpsimd.dma_start(out=rk[3:6, 0:N3], in_=U_gamma.partition_broadcast(3))
+        nc.gpsimd.dma_start(out=rk[6:7, 0 : 2 * H], in_=W_beta[0 : 2 * H].partition_broadcast(1))
+        nc.gpsimd.dma_start(out=rk[6:7, 3 * H : 4 * H], in_=W_beta[2 * H : N3].partition_broadcast(1))
+        nc.gpsimd.dma_start(out=rk[7:8, 0 : 2 * H], in_=b[0 : 2 * H].partition_broadcast(1))
+        nc.gpsimd.dma_start(out=rk[7:8, 3 * H : 4 * H], in_=b[2 * H : N3].partition_broadcast(1))
         nc.gpsimd.dma_start(out=rk[8:9, 0 : 2 * H], in_=U_beta[0 : 2 * H].partition_broadcast(1))
         nc.gpsimd.dma_start(out=rk[9:10, 2 * H : N3], in_=U_beta[2 * H : N3].partition_broadcast(1))
 
-        def regroup(src, grp):
+        def regroup(src, grp, first_bank):
             words = src[:].bitcast(F32)
             gview = grp[:].bitcast(F32).rearrange("p (g r u) -> p g r u", g=KG, r=P, u=2)
             for half in range(2):
-                xt = psaux.tile([P, 4, P], F32, name="xt", tag="aux")
+                xt = bank(first_bank + half, [P, 4, P], F32)
                 for gg in range(2):
                     g = 2 * half + gg
                     for u in range(2):
@@ -109,18 +111,18 @@ def tile_lngrucell_w_kernel(
                     in_=xt[:].rearrange("p (g u) r -> p g r u", g=2, u=2),
                 )
 
-        regroup(x_sb, grp_x)
-        regroup(h_sb, grp_h)
+        regroup(x_sb, grp_x, 0)
+        regroup(h_sb, grp_h, 2)
         nc.vector.quantize_mx(out=cod_x[:].bitcast(FP8X4), scales=pln_x[:], in_=grp_x[:])
         nc.vector.quantize_mx(out=cod_h[:].bitcast(FP8X4), scales=pln_h[:], in_=grp_h[:])
 
-        gt_ps = psaux.tile([P, P], BF16, name="gt_ps", tag="aux")
+        gt_ps = bank(4, [P, P], BF16)
         nc.tensor.transpose(out=gt_ps[:], in_=vecrows[:], identity=ident_b[:])
         nc.scalar.copy(out=g_t[:], in_=gt_ps[:])
 
         def spread(dst, first):
             for blk in range(6):
-                pg = psaux.tile([P, 1024], BF16, name="pg", tag="aux")
+                pg = bank(2 + (blk + 3) % 6, [P, 1024], BF16)
                 for i in range(8):
                     j = first + 8 * blk + i
                     nc.tensor.transpose(
@@ -135,7 +137,8 @@ def tile_lngrucell_w_kernel(
 
         def project(words, planes, cod, pln, gam, prod, stats, blocks):
             w32 = words.rearrange("g p n t -> p g (n t)").bitcast(I32)
-            bank = 0
+            count = 0
+            late = None
             for c0, width in blocks:
                 per = H // width
                 tiles = []
@@ -148,7 +151,7 @@ def tile_lngrucell_w_kernel(
                     tiles.append(wt)
                 for jj in range(width // NB):
                     n0 = c0 + NB * jj
-                    acc = psmx.tile([P, NB], F32, name="acc", tag="acc")
+                    acc = bank(count % 2, [P, NB], F32)
                     for g in range(KG):
                         lo = (g % per) * width + NB * jj
                         nc.tensor.matmul_mx(
@@ -160,89 +163,173 @@ def tile_lngrucell_w_kernel(
                             start=(g == 0),
                             stop=(g == KG - 1),
                         )
-                    nc.vector.bn_stats(out=stats[:, bank, :], in_=acc[:])
-                    nc.vector.tensor_tensor(
-                        out=prod[:, n0 : n0 + NB], in0=acc[:], in1=gam[:, n0 : n0 + NB], op=ALU.mult
-                    )
-                    bank += 1
+                    nc.vector.bn_stats(out=stats[:, count, :], in_=acc[:])
+                    count += 1
+                    if count == 12:
+                        late = (acc, n0)
+                    else:
+                        nc.vector.tensor_tensor(
+                            out=prod[:, n0 : n0 + NB], in0=acc[:], in1=gam[:, n0 : n0 + NB], op=ALU.mult
+                        )
+            return late
 
-        def ln_scalars(stats, csp, col, tagname):
+        def finish(late, gam, prod):
+            acc, n0 = late
+            nc.vector.tensor_tensor(out=prod[:, n0 : n0 + NB], in0=acc[:], in1=gam[:, n0 : n0 + NB], op=ALU.mult)
+
+        def ln_scalars(stats, col, tagname, late, gam, prod, ct_bank):
             mv = keep.tile([P, 2], F32, name="mv_" + tagname)
             ve = keep.tile([P, 1], F32, name="ve_" + tagname)
             rstd = keep.tile([P, 1], F32, name="rstd_" + tagname)
             shift = keep.tile([P, 1], F32, name="shift_" + tagname)
             rest = keep.tile([P, 1], F32, name="rest_" + tagname)
             lhs = keep.tile([P, P], BF16, name="lhs_" + tagname)
+            diag = keep.tile([P, P], F32, name="diag_" + tagname)
             nc.vector.bn_aggr(out=mv[:], in_=stats[:].rearrange("p j s -> p (j s)"))
             nc.vector.tensor_scalar_add(out=ve[:], in0=mv[:, 1:2], scalar1=EPS)
             nc.gpsimd.tensor_tensor(out=rstd[:], in0=ve[:], in1=neghalf[:], op=ALU.pow)
+            finish(late, gam, prod)
+            c1 = csp[:, col : col + 1]
+            c2 = csp[:, col + 1 : col + 2]
+            c3 = csp[:, col + 2 : col + 3]
             nc.vector.tensor_scalar(
                 out=shift[:], in0=mv[:, 0:1], scalar1=rstd[:, 0:1], scalar2=-1.0, op0=ALU.mult, op1=ALU.mult
             )
-            nc.vector.tensor_copy(out=csp[:, col : col + 1], in_=shift[:])
-            nc.vector.tensor_tensor(out=rest[:], in0=shift[:], in1=csp[:, col : col + 1], op=ALU.subtract)
-            nc.vector.tensor_copy(out=csp[:, col + 1 : col + 2], in_=rest[:])
-            nc.vector.tensor_tensor(
-                out=csp[:, col + 2 : col + 3], in0=rest[:], in1=csp[:, col + 1 : col + 2], op=ALU.subtract
+            nc.vector.tensor_scalar(
+                out=c1, in0=mv[:, 0:1], scalar1=rstd[:, 0:1], scalar2=-1.0, op0=ALU.mult, op1=ALU.mult
             )
-            ct = psaux.tile([P, P], BF16, name="ct", tag="aux")
+            nc.vector.tensor_scalar_mul(out=diag[:], in0=ident_f[:], scalar1=rstd[:, 0:1])
+            nc.vector.tensor_tensor(out=rest[:], in0=shift[:], in1=c1, op=ALU.subtract)
+            nc.vector.tensor_tensor(out=c2, in0=shift[:], in1=c1, op=ALU.subtract)
+            nc.vector.tensor_tensor(out=c3, in0=rest[:], in1=c2, op=ALU.subtract)
+            ct = bank(ct_bank, [P, P], BF16)
             nc.tensor.transpose(out=ct[:], in_=csp[:], identity=ident_b[:])
-            nc.vector.tensor_copy(out=lhs[:], in_=ct[:])
-            return rstd, lhs
+            nc.scalar.copy(out=lhs[:], in_=ct[:])
+            return rstd, shift, lhs, diag
 
-        def rank_terms(lhs, n0):
-            r_ps = psaux.tile([P, NB], F32, name="r_ps", tag="aux")
-            nc.tensor.matmul(out=r_ps[:], lhsT=lhs[:], rhs=rk[:, n0 : n0 + NB], start=True, stop=True)
-            return r_ps
+        def cs(gate, j):
+            return slice(gate * H + NB * j, gate * H + NB * (j + 1))
 
-        project(W_words, planes_w, cod_x, pln_x, g_w, p_w, st_w, [(0, H), (H, H), (2 * H, H)])
-        rstd_w, lhs_w = ln_scalars(st_w, csp_w, 0, "w")
-        for j in range(12):
-            n0 = NB * j
-            r_ps = rank_terms(lhs_w, n0)
-            nc.vector.scalar_tensor_tensor(
-                out=p_w[:, n0 : n0 + NB], in0=p_w[:, n0 : n0 + NB], scalar=rstd_w[:, 0:1], in1=r_ps[:],
-                op0=ALU.mult, op1=ALU.add,
-            )
+        def rank_pass(dst, lhs, col, start):
+            nc.tensor.matmul(out=dst[:], lhsT=lhs[:], rhs=rk[:, col : col + NB], start=start, stop=True)
 
-        project(
+        def scale_pass(dst, diag, src, start):
+            nc.tensor.matmul(out=dst[:], lhsT=diag[:], rhs=src, start=start, stop=False)
+
+        def stt(dst, in0, scalar, in1):
+            nc.vector.scalar_tensor_tensor(out=dst, in0=in0, scalar=scalar, in1=in1, op0=ALU.mult, op1=ALU.add)
+
+        def tt(dst, in0, in1, op):
+            nc.vector.tensor_tensor(out=dst, in0=in0, in1=in1, op=op)
+
+        late_w = project(W_words, planes_w, cod_x, pln_x, g_w, p_w, st_w, [(0, H), (H, H), (2 * H, H)])
+        rstd_w, shift_w, lhs_w, diag_w = ln_scalars(st_w, 0, "w", late_w, g_w, p_w, 2)
+        sw = rstd_w[:, 0:1]
+        for i, (col, dst) in enumerate(
+            [(3 * H + NB * j, cs(2, j)) for j in range(4)] + [(H, cs(1, 0))]
+        ):
+            r_ps = bank(3 + i, [P, NB], F32)
+            rank_pass(r_ps, lhs_w, col, True)
+            stt(p_w[:, dst], p_w[:, dst], sw, r_ps[:])
+        d1 = [None]
+        for j in range(1, 4):
+            d = bank(1 + j, [P, NB], F32)
+            scale_pass(d, diag_w, p_w[:, cs(1, j)], True)
+            d1.append(d)
+        d0 = []
+        for j in range(3):
+            d = bank(5 + j, [P, NB], F32)
+            scale_pass(d, diag_w, p_w[:, cs(0, j)], True)
+            d0.append(d)
+
+        late_u = project(
             U_words, planes_u, cod_h, pln_h, g_u, p_u, st_u,
             [(H, H), (2 * H, H), (0, 1024), (1024, NB), (1536, NB)],
         )
-        rstd_u, lhs_u = ln_scalars(st_u, csp_u, 3, "u")
 
-        for j in range(4):
-            c1 = slice(H + NB * j, H + NB * (j + 1))
-            nc.vector.scalar_tensor_tensor(
-                out=p_u[:, c1], in0=p_u[:, c1], scalar=rstd_u[:, 0:1], in1=p_w[:, c1], op0=ALU.mult, op1=ALU.add
-            )
-        for j in range(4):
-            c1 = slice(H + NB * j, H + NB * (j + 1))
-            r_ps = rank_terms(lhs_u, H + NB * j)
-            nc.vector.tensor_tensor(out=p_u[:, c1], in0=p_u[:, c1], in1=r_ps[:], op=ALU.add)
-            nc.scalar.activation(out=p_u[:, c1], in_=p_u[:, c1], func=ACT.Sigmoid)
-        for j in range(4):
-            c1 = slice(H + NB * j, H + NB * (j + 1))
-            c2 = slice(2 * H + NB * j, 2 * H + NB * (j + 1))
-            r_ps = rank_terms(lhs_u, 2 * H + NB * j)
-            nc.vector.scalar_tensor_tensor(
-                out=p_u[:, c2], in0=p_u[:, c2], scalar=rstd_u[:, 0:1], in1=r_ps[:], op0=ALU.mult, op1=ALU.add
-            )
-            nc.vector.tensor_tensor(out=p_u[:, c2], in0=p_u[:, c2], in1=p_u[:, c1], op=ALU.mult)
-            nc.vector.tensor_tensor(out=p_u[:, c2], in0=p_u[:, c2], in1=p_w[:, c2], op=ALU.add)
-            nc.scalar.activation(out=p_u[:, c2], in_=p_u[:, c2], func=ACT.Tanh)
-        for j in range(4):
-            c0 = slice(NB * j, NB * (j + 1))
-            r_ps = rank_terms(lhs_u, NB * j)
-            nc.vector.scalar_tensor_tensor(
-                out=p_u[:, c0], in0=p_u[:, c0], scalar=rstd_u[:, 0:1], in1=p_w[:, c0], op0=ALU.mult, op1=ALU.add
-            )
-            nc.vector.tensor_tensor(out=p_u[:, c0], in0=p_u[:, c0], in1=r_ps[:], op=ALU.add)
-            nc.scalar.activation(out=p_u[:, c0], in_=p_u[:, c0], func=ACT.Sigmoid)
-        for j in range(4):
-            c0 = slice(NB * j, NB * (j + 1))
-            c2 = slice(2 * H + NB * j, 2 * H + NB * (j + 1))
-            nc.vector.tensor_tensor(out=p_w[:, c0], in0=h_sb[:, c0], in1=p_u[:, c2], op=ALU.subtract)
-            nc.vector.tensor_tensor(out=p_w[:, c0], in0=p_w[:, c0], in1=p_u[:, c0], op=ALU.mult)
-            nc.vector.tensor_tensor(out=p_w[:, c0], in0=p_w[:, c0], in1=p_u[:, c2], op=ALU.add)
-            nc.sync.dma_start(out=out[:, c0], in_=p_w[:, c0])
+        ctx.enter_context(tc.manual_schedule())
+        d = bank(0, [P, NB], F32)
+        scale_pass(d, diag_w, p_w[:, cs(0, 3)], True)
+        d0.append(d)
+        rstd_u, shift_u, lhs_a, diag_u = ln_scalars(st_u, 3, "u", late_u, g_u, p_u, 1)
+        su = rstd_u[:, 0:1]
+        h2 = [None] * 4
+
+        def reset_gate(j):
+            nc.scalar.activation(out=p_u[:, cs(1, j)], in_=p_u[:, cs(1, j)], func=ACT.Sigmoid)
+
+        def reset_arg(j):
+            rank_pass(d1[j], lhs_a, H + NB * j, False)
+            stt(p_u[:, cs(1, j)], p_u[:, cs(1, j)], su, d1[j][:])
+
+        def hidden(j, where):
+            h2[j] = bank(where, [P, NB], F32)
+            scale_pass(h2[j], diag_u, p_u[:, cs(2, j)], True)
+            rank_pass(h2[j], lhs_a, 2 * H + NB * j, False)
+
+        def gated(j):
+            tt(p_u[:, cs(2, j)], p_u[:, cs(1, j)], h2[j][:], ALU.mult)
+
+        def cand_arg(j):
+            tt(p_u[:, cs(2, j)], p_u[:, cs(2, j)], p_w[:, cs(2, j)], ALU.add)
+
+        def cand(j):
+            nc.scalar.activation(out=p_u[:, cs(2, j)], in_=p_u[:, cs(2, j)], func=ACT.Tanh)
+
+        def update(j):
+            scale_pass(d0[j], diag_u, p_u[:, cs(0, j)], False)
+            rank_pass(d0[j], lhs_a, NB * j, False)
+            nc.scalar.activation(out=p_u[:, cs(0, j)], in_=d0[j][:], func=ACT.Sigmoid)
+
+        def diff(j):
+            tt(p_w[:, cs(0, j)], h_sb[:, cs(0, j)], p_u[:, cs(2, j)], ALU.subtract)
+
+        def weigh(j):
+            tt(p_w[:, cs(0, j)], p_w[:, cs(0, j)], p_u[:, cs(0, j)], ALU.mult)
+
+        def blend(j):
+            tt(p_w[:, cs(0, j)], p_w[:, cs(0, j)], p_u[:, cs(2, j)], ALU.add)
+            nc.sync.dma_start(out=out[:, cs(0, j)], in_=p_w[:, cs(0, j)])
+
+        stt(p_u[:, cs(1, 0)], p_u[:, cs(1, 0)], su, p_w[:, cs(1, 0)])
+        stt(p_u[:, cs(1, 0)], g_u[:, cs(1, 0)], shift_u[:, 0:1], p_u[:, cs(1, 0)])
+        reset_gate(0)
+        reset_arg(1)
+        reset_gate(1)
+        reset_arg(2)
+        reset_gate(2)
+        rank_pass(d1[3], lhs_a, H + NB * 3, False)
+        hidden(0, 1)
+        gated(0)
+        stt(p_u[:, cs(1, 3)], p_u[:, cs(1, 3)], su, d1[3][:])
+        reset_gate(3)
+        cand_arg(0)
+        cand(0)
+        hidden(1, 2)
+        gated(1)
+        cand_arg(1)
+        update(0)
+        cand(1)
+        diff(0)
+        hidden(2, 3)
+        gated(2)
+        weigh(0)
+        cand_arg(2)
+        blend(0)
+        update(1)
+        cand(2)
+        diff(1)
+        hidden(3, 4)
+        gated(3)
+        weigh(1)
+        cand_arg(3)
+        blend(1)
+        update(2)
+        cand(3)
+        update(3)
+        diff(2)
+        diff(3)
+        weigh(2)
+        weigh(3)
+        blend(2)
+        blend(3)

@@ -28,6 +28,7 @@ def tile_lngrucell_w_kernel(
         keep = ctx.enter_context(tc.tile_pool(name="keep", bufs=1))
         wpool = ctx.enter_context(tc.tile_pool(name="wpool", bufs=12))
         psum = ctx.enter_context(tc.psum_pool(name="psum", bufs=1))
+        ctx.enter_context(tc.manual_schedule())
 
         def bank(i, shape, dtype):
             return psum.tile(shape, dtype, name="ps%d" % i, tag="b%d" % i)
@@ -112,34 +113,37 @@ def tile_lngrucell_w_kernel(
                 )
 
         regroup(x_sb, grp_x, 0)
-        regroup(h_sb, grp_h, 2)
         nc.vector.quantize_mx(out=cod_x[:].bitcast(FP8X4), scales=pln_x[:], in_=grp_x[:])
-        nc.vector.quantize_mx(out=cod_h[:].bitcast(FP8X4), scales=pln_h[:], in_=grp_h[:])
 
-        gt_ps = bank(4, [P, P], BF16)
+        gt_ps = bank(2, [P, P], BF16)
         nc.tensor.transpose(out=gt_ps[:], in_=vecrows[:], identity=ident_b[:])
         nc.scalar.copy(out=g_t[:], in_=gt_ps[:])
 
-        def spread(dst, first):
-            for blk in range(6):
-                pg = bank(2 + (blk + 3) % 6, [P, 1024], BF16)
-                for i in range(8):
-                    j = first + 8 * blk + i
+        def spread(dst, first, blocks, share):
+            for blk in blocks:
+                pg = bank(3 + blk % 5, [P, NB], BF16)
+                for i in range(4):
+                    j = first + 4 * blk + i
                     nc.tensor.transpose(
                         out=pg[:, P * i : P * (i + 1)],
                         in_=g_t[:, j : j + 1].to_broadcast([P, P]),
                         identity=ident_b[:],
                     )
-                nc.scalar.copy(out=dst[:, 1024 * blk : 1024 * (blk + 1)], in_=pg[:])
+                if share and blk % 2 == 0:
+                    nc.vector.tensor_copy(out=dst[:, NB * blk : NB * (blk + 1)], in_=pg[:])
+                else:
+                    nc.scalar.copy(out=dst[:, NB * blk : NB * (blk + 1)], in_=pg[:])
 
-        spread(g_w, 0)
-        spread(g_u, 48)
+        spread(g_w, 0, range(12), True)
+        regroup(h_sb, grp_h, 0)
+        nc.vector.quantize_mx(out=cod_h[:].bitcast(FP8X4), scales=pln_h[:], in_=grp_h[:])
+        spread(g_u, 48, range(0, 6), False)
 
-        def project(words, planes, cod, pln, gam, prod, stats, blocks):
+        def project(words, planes, cod, pln, gam, prod, stats, blocks, after):
             w32 = words.rearrange("g p n t -> p g (n t)").bitcast(I32)
             count = 0
             late = None
-            for c0, width in blocks:
+            for index, (c0, width) in enumerate(blocks):
                 per = H // width
                 tiles = []
                 for t in range(KG // per):
@@ -151,7 +155,7 @@ def tile_lngrucell_w_kernel(
                     tiles.append(wt)
                 for jj in range(width // NB):
                     n0 = c0 + NB * jj
-                    acc = bank(count % 2, [P, NB], F32)
+                    acc = bank(count % 3, [P, NB], F32)
                     for g in range(KG):
                         lo = (g % per) * width + NB * jj
                         nc.tensor.matmul_mx(
@@ -171,13 +175,15 @@ def tile_lngrucell_w_kernel(
                         nc.vector.tensor_tensor(
                             out=prod[:, n0 : n0 + NB], in0=acc[:], in1=gam[:, n0 : n0 + NB], op=ALU.mult
                         )
+                if index in after:
+                    after[index]()
             return late
 
         def finish(late, gam, prod):
             acc, n0 = late
             nc.vector.tensor_tensor(out=prod[:, n0 : n0 + NB], in0=acc[:], in1=gam[:, n0 : n0 + NB], op=ALU.mult)
 
-        def ln_scalars(stats, col, tagname, late, gam, prod, ct_bank):
+        def ln_scalars(stats, col, tagname, late, gam, prod, ct_bank, early):
             mv = keep.tile([P, 2], F32, name="mv_" + tagname)
             ve = keep.tile([P, 1], F32, name="ve_" + tagname)
             rstd = keep.tile([P, 1], F32, name="rstd_" + tagname)
@@ -199,6 +205,7 @@ def tile_lngrucell_w_kernel(
                 out=c1, in0=mv[:, 0:1], scalar1=rstd[:, 0:1], scalar2=-1.0, op0=ALU.mult, op1=ALU.mult
             )
             nc.vector.tensor_scalar_mul(out=diag[:], in0=ident_f[:], scalar1=rstd[:, 0:1])
+            early(diag)
             nc.vector.tensor_tensor(out=rest[:], in0=shift[:], in1=c1, op=ALU.subtract)
             nc.vector.tensor_tensor(out=c2, in0=shift[:], in1=c1, op=ALU.subtract)
             nc.vector.tensor_tensor(out=c3, in0=rest[:], in1=c2, op=ALU.subtract)
@@ -222,36 +229,44 @@ def tile_lngrucell_w_kernel(
         def tt(dst, in0, in1, op):
             nc.vector.tensor_tensor(out=dst, in0=in0, in1=in1, op=op)
 
-        late_w = project(W_words, planes_w, cod_x, pln_x, g_w, p_w, st_w, [(0, H), (H, H), (2 * H, H)])
-        rstd_w, shift_w, lhs_w, diag_w = ln_scalars(st_w, 0, "w", late_w, g_w, p_w, 2)
+        late_w = project(
+            W_words, planes_w, cod_x, pln_x, g_w, p_w, st_w, [(0, H), (H, H), (2 * H, H)],
+            {0: lambda: spread(g_u, 48, range(6, 9), False), 1: lambda: spread(g_u, 48, range(9, 12), False)},
+        )
+        d1 = [None]
+        d0 = []
+
+        def open_group(held, diag, gate, j, where):
+            d = bank(where, [P, NB], F32)
+            scale_pass(d, diag, p_w[:, cs(gate, j)], True)
+            held.append(d)
+
+        def open_first(diag):
+            open_group(d1, diag, 1, 1, 3)
+            open_group(d1, diag, 1, 2, 4)
+
+        rstd_w, shift_w, lhs_w, diag_w = ln_scalars(st_w, 0, "w", late_w, g_w, p_w, 5, open_first)
         sw = rstd_w[:, 0:1]
         for i, (col, dst) in enumerate(
             [(3 * H + NB * j, cs(2, j)) for j in range(4)] + [(H, cs(1, 0))]
         ):
-            r_ps = bank(3 + i, [P, NB], F32)
+            r_ps = bank(5 + (i + 1) % 3, [P, NB], F32)
             rank_pass(r_ps, lhs_w, col, True)
             stt(p_w[:, dst], p_w[:, dst], sw, r_ps[:])
-        d1 = [None]
-        for j in range(1, 4):
-            d = bank(1 + j, [P, NB], F32)
-            scale_pass(d, diag_w, p_w[:, cs(1, j)], True)
-            d1.append(d)
-        d0 = []
-        for j in range(3):
-            d = bank(5 + j, [P, NB], F32)
-            scale_pass(d, diag_w, p_w[:, cs(0, j)], True)
-            d0.append(d)
+        def open_rest():
+            open_group(d1, diag_w, 1, 3, 5)
+            open_group(d0, diag_w, 0, 0, 6)
+            open_group(d0, diag_w, 0, 1, 7)
 
         late_u = project(
             U_words, planes_u, cod_h, pln_h, g_u, p_u, st_u,
             [(H, H), (2 * H, H), (0, 1024), (1024, NB), (1536, NB)],
+            {0: open_rest},
         )
 
-        ctx.enter_context(tc.manual_schedule())
-        d = bank(0, [P, NB], F32)
-        scale_pass(d, diag_w, p_w[:, cs(0, 3)], True)
-        d0.append(d)
-        rstd_u, shift_u, lhs_a, diag_u = ln_scalars(st_u, 3, "u", late_u, g_u, p_u, 1)
+        open_group(d0, diag_w, 0, 2, 0)
+        open_group(d0, diag_w, 0, 3, 1)
+        rstd_u, shift_u, lhs_a, diag_u = ln_scalars(st_u, 3, "u", late_u, g_u, p_u, 2, lambda diag: None)
         su = rstd_u[:, 0:1]
         h2 = [None] * 4
 
@@ -299,19 +314,19 @@ def tile_lngrucell_w_kernel(
         reset_arg(2)
         reset_gate(2)
         rank_pass(d1[3], lhs_a, H + NB * 3, False)
-        hidden(0, 1)
+        hidden(0, 2)
         gated(0)
         stt(p_u[:, cs(1, 3)], p_u[:, cs(1, 3)], su, d1[3][:])
         reset_gate(3)
         cand_arg(0)
         cand(0)
-        hidden(1, 2)
+        hidden(1, 3)
         gated(1)
         cand_arg(1)
         update(0)
         cand(1)
         diff(0)
-        hidden(2, 3)
+        hidden(2, 4)
         gated(2)
         weigh(0)
         cand_arg(2)
@@ -319,7 +334,7 @@ def tile_lngrucell_w_kernel(
         update(1)
         cand(2)
         diff(1)
-        hidden(3, 4)
+        hidden(3, 5)
         gated(3)
         weigh(1)
         cand_arg(3)

@@ -61,6 +61,7 @@ def tile_lngrucell_w_kernel(
 
         nc.vector.memset(planes_w[:].bitcast(I32), 0)
         nc.vector.memset(planes_u[:].bitcast(I32), 0)
+        nc.vector.memset(rk[:].bitcast(I32), 0)
         nc.vector.memset(warm_in[:], 0.0)
         nc.vector.memset(neghalf[:], -0.5)
         nc.vector.memset(csp[:], 0.0)
@@ -68,22 +69,23 @@ def tile_lngrucell_w_kernel(
 
         nc.sync.dma_start(out=x_sb[:], in_=x_in)
         nc.sync.dma_start(out=h_sb[:], in_=hx)
-        for planes, scales in ((planes_w, W_scales), (planes_u, U_scales)):
-            s32 = scales.bitcast(I32)
-            for q in range(4):
-                nc.sync.dma_start(
-                    out=planes[32 * q : 32 * q + 16, :].bitcast(I32),
-                    in_=s32[:, 4 * q : 4 * q + 4, :],
-                )
-
         nc.scalar.dma_start(out=vecrows[0:48, :], in_=W_gamma.rearrange("(j p) -> j p", p=P))
         nc.scalar.dma_start(out=vecrows[48:96, :], in_=U_gamma.rearrange("(j p) -> j p", p=P))
         nc.scalar.dma_start(out=vecrows[96:128, :], in_=W_beta[0:4096].rearrange("(j p) -> j p", p=P))
+        for planes, scales in ((planes_w, W_scales), (planes_u, U_scales)):
+            for q in range(2):
+                nc.sync.dma_start(
+                    out=planes[32 * q : 32 * q + 16, :].bitcast(I32),
+                    in_=scales.bitcast(I32)[:, 4 * q : 4 * q + 4, :],
+                )
+                nc.scalar.dma_start(
+                    out=planes[32 * q + 64 : 32 * q + 80, :].bitcast(F32),
+                    in_=scales.bitcast(F32)[:, 4 * q + 8 : 4 * q + 12, :],
+                )
         nc.scalar.activation(out=warm_out[:], in_=warm_in[:], func=ACT.Sigmoid)
 
         make_identity(nc, ident_f[:])
         make_identity(nc, ident_b[:])
-        nc.gpsimd.memset(rk[:].bitcast(F32), 0.0)
         nc.gpsimd.dma_start(out=rk[0:3, 0 : 2 * H], in_=W_gamma[0 : 2 * H].partition_broadcast(3))
         nc.gpsimd.dma_start(out=rk[0:3, 3 * H : 4 * H], in_=W_gamma[2 * H : N3].partition_broadcast(3))
         nc.gpsimd.dma_start(out=rk[3:6, 0:N3], in_=U_gamma.partition_broadcast(3))
@@ -230,7 +232,8 @@ def tile_lngrucell_w_kernel(
             nc.vector.tensor_tensor(out=dst, in0=in0, in1=in1, op=op)
 
         late_w = project(
-            W_words, planes_w, cod_x, pln_x, g_w, p_w, st_w, [(0, H), (H, H), (2 * H, H)],
+            W_words, planes_w, cod_x, pln_x, g_w, p_w, st_w,
+            [(0, H), (H, H), (2 * H, 1024), (2 * H + 1024, NB), (2 * H + 1536, NB)],
             {0: lambda: spread(g_u, 48, range(6, 9), False), 1: lambda: spread(g_u, 48, range(9, 12), False)},
         )
         d1 = [None]
@@ -245,23 +248,22 @@ def tile_lngrucell_w_kernel(
             open_group(d1, diag, 1, 1, 3)
             open_group(d1, diag, 1, 2, 4)
 
-        rstd_w, shift_w, lhs_w, diag_w = ln_scalars(st_w, 0, "w", late_w, g_w, p_w, 5, open_first)
+        rstd_w, shift_w, lhs_w, diag_w = ln_scalars(st_w, 0, "w", late_w, g_w, p_w, 0, open_first)
+        open_group(d1, diag_w, 1, 3, 5)
+        open_group(d0, diag_w, 0, 0, 6)
+        open_group(d0, diag_w, 0, 1, 7)
         sw = rstd_w[:, 0:1]
         for i, (col, dst) in enumerate(
             [(3 * H + NB * j, cs(2, j)) for j in range(4)] + [(H, cs(1, 0))]
         ):
-            r_ps = bank(5 + (i + 1) % 3, [P, NB], F32)
+            r_ps = bank((i + 1) % 3, [P, NB], F32)
             rank_pass(r_ps, lhs_w, col, True)
             stt(p_w[:, dst], p_w[:, dst], sw, r_ps[:])
-        def open_rest():
-            open_group(d1, diag_w, 1, 3, 5)
-            open_group(d0, diag_w, 0, 0, 6)
-            open_group(d0, diag_w, 0, 1, 7)
 
         late_u = project(
             U_words, planes_u, cod_h, pln_h, g_u, p_u, st_u,
             [(H, H), (2 * H, H), (0, 1024), (1024, NB), (1536, NB)],
-            {0: open_rest},
+            {},
         )
 
         open_group(d0, diag_w, 0, 2, 0)

@@ -145,13 +145,12 @@ def tile_lngrucell_w_kernel(
             w32 = words.rearrange("g p n t -> p g (n t)").bitcast(I32)
             count = 0
             late = None
-            for index, (c0, width) in enumerate(blocks):
-                per = H // width
+            for index, (c0, width, per) in enumerate(blocks):
                 tiles = []
                 for t in range(KG // per):
                     wt = wpool.tile([P, H], I32, name="wt", tag="wt", align_bytes=64)
                     nc.sync.dma_start(
-                        out=wt[:].rearrange("p (g n) -> p g n", g=per),
+                        out=wt[:, 0 : per * width].rearrange("p (g n) -> p g n", g=per),
                         in_=w32[:, t * per : (t + 1) * per, c0 : c0 + width],
                     )
                     tiles.append(wt)
@@ -197,6 +196,8 @@ def tile_lngrucell_w_kernel(
             nc.vector.tensor_scalar_add(out=ve[:], in0=mv[:, 1:2], scalar1=EPS)
             nc.gpsimd.tensor_tensor(out=rstd[:], in0=ve[:], in1=neghalf[:], op=ALU.pow)
             finish(late, gam, prod)
+            nc.scalar.activation(out=diag[:], in_=ident_f[:], func=ACT.Copy, scale=rstd[:, 0:1])
+            early(diag)
             c1 = csp[:, col : col + 1]
             c2 = csp[:, col + 1 : col + 2]
             c3 = csp[:, col + 2 : col + 3]
@@ -206,8 +207,6 @@ def tile_lngrucell_w_kernel(
             nc.vector.tensor_scalar(
                 out=c1, in0=mv[:, 0:1], scalar1=rstd[:, 0:1], scalar2=-1.0, op0=ALU.mult, op1=ALU.mult
             )
-            nc.vector.tensor_scalar_mul(out=diag[:], in0=ident_f[:], scalar1=rstd[:, 0:1])
-            early(diag)
             nc.vector.tensor_tensor(out=rest[:], in0=shift[:], in1=c1, op=ALU.subtract)
             nc.vector.tensor_tensor(out=c2, in0=shift[:], in1=c1, op=ALU.subtract)
             nc.vector.tensor_tensor(out=c3, in0=rest[:], in1=c2, op=ALU.subtract)
@@ -233,10 +232,10 @@ def tile_lngrucell_w_kernel(
 
         late_w = project(
             W_words, planes_w, cod_x, pln_x, g_w, p_w, st_w,
-            [(0, H), (H, H), (2 * H, 1024), (2 * H + 1024, NB), (2 * H + 1536, NB)],
+            [(0, H, 1), (H, H, 1), (2 * H, 1024, 2), (2 * H + 1024, NB, 4), (2 * H + 1536, NB, 4)],
             {0: lambda: spread(g_u, 48, range(6, 9), False), 1: lambda: spread(g_u, 48, range(9, 12), False)},
         )
-        d1 = [None]
+        d1 = [None, None]
         d0 = []
 
         def open_group(held, diag, gate, j, where):
@@ -245,16 +244,15 @@ def tile_lngrucell_w_kernel(
             held.append(d)
 
         def open_first(diag):
-            open_group(d1, diag, 1, 1, 3)
             open_group(d1, diag, 1, 2, 4)
+            open_group(d1, diag, 1, 3, 5)
 
         rstd_w, shift_w, lhs_w, diag_w = ln_scalars(st_w, 0, "w", late_w, g_w, p_w, 0, open_first)
-        open_group(d1, diag_w, 1, 3, 5)
         open_group(d0, diag_w, 0, 0, 6)
         open_group(d0, diag_w, 0, 1, 7)
         sw = rstd_w[:, 0:1]
         for i, (col, dst) in enumerate(
-            [(3 * H + NB * j, cs(2, j)) for j in range(4)] + [(H, cs(1, 0))]
+            [(3 * H + NB * j, cs(2, j)) for j in range(4)] + [(H, cs(1, 0)), (H + NB, cs(1, 1))]
         ):
             r_ps = bank((i + 1) % 3, [P, NB], F32)
             rank_pass(r_ps, lhs_w, col, True)
@@ -262,27 +260,32 @@ def tile_lngrucell_w_kernel(
 
         late_u = project(
             U_words, planes_u, cod_h, pln_h, g_u, p_u, st_u,
-            [(H, H), (2 * H, H), (0, 1024), (1024, NB), (1536, NB)],
+            [(H, H, 1), (2 * H, H, 1), (0, 1024, 2), (1024, NB, 4), (1536, NB, 1)],
             {},
         )
 
         open_group(d0, diag_w, 0, 2, 0)
         open_group(d0, diag_w, 0, 3, 1)
-        rstd_u, shift_u, lhs_a, diag_u = ln_scalars(st_u, 3, "u", late_u, g_u, p_u, 2, lambda diag: None)
-        su = rstd_u[:, 0:1]
         h2 = [None] * 4
+
+        def hidden_scale(j, where, diag):
+            h2[j] = bank(where, [P, NB], F32)
+            scale_pass(h2[j], diag, p_u[:, cs(2, j)], True)
+
+        rstd_u, shift_u, lhs_a, diag_u = ln_scalars(
+            st_u, 3, "u", late_u, g_u, p_u, 2, lambda diag: hidden_scale(0, 3, diag)
+        )
+        su = rstd_u[:, 0:1]
+
+        def hidden_rank(j):
+            rank_pass(h2[j], lhs_a, 2 * H + NB * j, False)
+
+        def hidden(j, where):
+            hidden_scale(j, where, diag_u)
+            hidden_rank(j)
 
         def reset_gate(j):
             nc.scalar.activation(out=p_u[:, cs(1, j)], in_=p_u[:, cs(1, j)], func=ACT.Sigmoid)
-
-        def reset_arg(j):
-            rank_pass(d1[j], lhs_a, H + NB * j, False)
-            stt(p_u[:, cs(1, j)], p_u[:, cs(1, j)], su, d1[j][:])
-
-        def hidden(j, where):
-            h2[j] = bank(where, [P, NB], F32)
-            scale_pass(h2[j], diag_u, p_u[:, cs(2, j)], True)
-            rank_pass(h2[j], lhs_a, 2 * H + NB * j, False)
 
         def gated(j):
             tt(p_u[:, cs(2, j)], p_u[:, cs(1, j)], h2[j][:], ALU.mult)
@@ -308,21 +311,22 @@ def tile_lngrucell_w_kernel(
             tt(p_w[:, cs(0, j)], p_w[:, cs(0, j)], p_u[:, cs(2, j)], ALU.add)
             nc.sync.dma_start(out=out[:, cs(0, j)], in_=p_w[:, cs(0, j)])
 
-        stt(p_u[:, cs(1, 0)], p_u[:, cs(1, 0)], su, p_w[:, cs(1, 0)])
-        stt(p_u[:, cs(1, 0)], g_u[:, cs(1, 0)], shift_u[:, 0:1], p_u[:, cs(1, 0)])
-        reset_gate(0)
-        reset_arg(1)
-        reset_gate(1)
-        reset_arg(2)
+        for j in range(2):
+            stt(p_u[:, cs(1, j)], p_u[:, cs(1, j)], su, p_w[:, cs(1, j)])
+        for j in range(2):
+            stt(p_u[:, cs(1, j)], g_u[:, cs(1, j)], shift_u[:, 0:1], p_u[:, cs(1, j)])
+            reset_gate(j)
+        rank_pass(d1[2], lhs_a, H + NB * 2, False)
+        stt(p_u[:, cs(1, 2)], p_u[:, cs(1, 2)], su, d1[2][:])
         reset_gate(2)
         rank_pass(d1[3], lhs_a, H + NB * 3, False)
-        hidden(0, 2)
+        hidden_rank(0)
         gated(0)
         stt(p_u[:, cs(1, 3)], p_u[:, cs(1, 3)], su, d1[3][:])
         reset_gate(3)
         cand_arg(0)
         cand(0)
-        hidden(1, 3)
+        hidden(1, 2)
         gated(1)
         cand_arg(1)
         update(0)

@@ -72,20 +72,24 @@ def tile_lngrucell_w_kernel(
         nc.scalar.dma_start(out=vecrows[0:48, :], in_=W_gamma.rearrange("(j p) -> j p", p=P))
         nc.scalar.dma_start(out=vecrows[48:96, :], in_=U_gamma.rearrange("(j p) -> j p", p=P))
         nc.scalar.dma_start(out=vecrows[96:128, :], in_=W_beta[0:4096].rearrange("(j p) -> j p", p=P))
-        for planes, scales in ((planes_w, W_scales), (planes_u, U_scales)):
-            for q in range(2):
-                nc.sync.dma_start(
-                    out=planes[32 * q : 32 * q + 16, :].bitcast(I32),
-                    in_=scales.bitcast(I32)[:, 4 * q : 4 * q + 4, :],
-                )
-                nc.scalar.dma_start(
-                    out=planes[32 * q + 64 : 32 * q + 80, :].bitcast(F32),
-                    in_=scales.bitcast(F32)[:, 4 * q + 8 : 4 * q + 12, :],
-                )
+        for q in range(2):
+            nc.sync.dma_start(
+                out=planes_w[32 * q : 32 * q + 16, :].bitcast(I32),
+                in_=W_scales.bitcast(I32)[:, 4 * q : 4 * q + 4, :],
+            )
+            nc.scalar.dma_start(
+                out=planes_w[32 * q + 64 : 32 * q + 80, :].bitcast(F32),
+                in_=W_scales.bitcast(F32)[:, 4 * q + 8 : 4 * q + 12, :],
+            )
         nc.scalar.activation(out=warm_out[:], in_=warm_in[:], func=ACT.Sigmoid)
 
         make_identity(nc, ident_f[:])
         make_identity(nc, ident_b[:])
+        for q in range(4):
+            nc.gpsimd.dma_start(
+                out=planes_u[32 * q : 32 * q + 16, :].bitcast(F32),
+                in_=U_scales.bitcast(F32)[:, 4 * q : 4 * q + 4, :],
+            )
         nc.gpsimd.dma_start(out=rk[0:3, 0 : 2 * H], in_=W_gamma[0 : 2 * H].partition_broadcast(3))
         nc.gpsimd.dma_start(out=rk[0:3, 3 * H : 4 * H], in_=W_gamma[2 * H : N3].partition_broadcast(3))
         nc.gpsimd.dma_start(out=rk[3:6, 0:N3], in_=U_gamma.partition_broadcast(3))

@@ -72,24 +72,17 @@ def tile_lngrucell_w_kernel(
         nc.scalar.dma_start(out=vecrows[0:48, :], in_=W_gamma.rearrange("(j p) -> j p", p=P))
         nc.scalar.dma_start(out=vecrows[48:96, :], in_=U_gamma.rearrange("(j p) -> j p", p=P))
         nc.scalar.dma_start(out=vecrows[96:128, :], in_=W_beta[0:4096].rearrange("(j p) -> j p", p=P))
-        for q in range(2):
-            nc.sync.dma_start(
-                out=planes_w[32 * q : 32 * q + 16, :].bitcast(I32),
-                in_=W_scales.bitcast(I32)[:, 4 * q : 4 * q + 4, :],
-            )
-            nc.scalar.dma_start(
-                out=planes_w[32 * q + 64 : 32 * q + 80, :].bitcast(F32),
-                in_=W_scales.bitcast(F32)[:, 4 * q + 8 : 4 * q + 12, :],
-            )
         nc.scalar.activation(out=warm_out[:], in_=warm_in[:], func=ACT.Sigmoid)
 
         make_identity(nc, ident_f[:])
-        make_identity(nc, ident_b[:])
-        for q in range(4):
-            nc.gpsimd.dma_start(
-                out=planes_u[32 * q : 32 * q + 16, :].bitcast(F32),
-                in_=U_scales.bitcast(F32)[:, 4 * q : 4 * q + 4, :],
-            )
+        for planes, scales in ((planes_w, W_scales), (planes_u, U_scales)):
+            for q in range(4):
+                nc.gpsimd.dma_start(
+                    out=planes[32 * q : 32 * q + 16, :].bitcast(F32),
+                    in_=scales.bitcast(F32)[:, 4 * q : 4 * q + 4, :],
+                )
+            if planes is planes_w:
+                make_identity(nc, ident_b[:])
         nc.gpsimd.dma_start(out=rk[0:3, 0 : 2 * H], in_=W_gamma[0 : 2 * H].partition_broadcast(3))
         nc.gpsimd.dma_start(out=rk[0:3, 3 * H : 4 * H], in_=W_gamma[2 * H : N3].partition_broadcast(3))
         nc.gpsimd.dma_start(out=rk[3:6, 0:N3], in_=U_gamma.partition_broadcast(3))

@@ -74,24 +74,27 @@ def tile_lngrucell_w_kernel(
         nc.scalar.dma_start(out=vecrows[96:128, :], in_=W_beta[0:4096].rearrange("(j p) -> j p", p=P))
         nc.scalar.activation(out=warm_out[:], in_=warm_in[:], func=ACT.Sigmoid)
 
-        make_identity(nc, ident_f[:])
-        for planes, scales in ((planes_w, W_scales), (planes_u, U_scales)):
+        def load_scales(planes, scales):
             for q in range(4):
                 nc.gpsimd.dma_start(
                     out=planes[32 * q : 32 * q + 16, :].bitcast(F32),
                     in_=scales.bitcast(F32)[:, 4 * q : 4 * q + 4, :],
                 )
-            if planes is planes_w:
-                make_identity(nc, ident_b[:])
-        nc.gpsimd.dma_start(out=rk[0:3, 0 : 2 * H], in_=W_gamma[0 : 2 * H].partition_broadcast(3))
-        nc.gpsimd.dma_start(out=rk[0:3, 3 * H : 4 * H], in_=W_gamma[2 * H : N3].partition_broadcast(3))
-        nc.gpsimd.dma_start(out=rk[3:6, 0:N3], in_=U_gamma.partition_broadcast(3))
-        nc.gpsimd.dma_start(out=rk[6:7, 0 : 2 * H], in_=W_beta[0 : 2 * H].partition_broadcast(1))
-        nc.gpsimd.dma_start(out=rk[6:7, 3 * H : 4 * H], in_=W_beta[2 * H : N3].partition_broadcast(1))
-        nc.gpsimd.dma_start(out=rk[7:8, 0 : 2 * H], in_=b[0 : 2 * H].partition_broadcast(1))
-        nc.gpsimd.dma_start(out=rk[7:8, 3 * H : 4 * H], in_=b[2 * H : N3].partition_broadcast(1))
-        nc.gpsimd.dma_start(out=rk[8:9, 0 : 2 * H], in_=U_beta[0 : 2 * H].partition_broadcast(1))
-        nc.gpsimd.dma_start(out=rk[9:10, 2 * H : N3], in_=U_beta[2 * H : N3].partition_broadcast(1))
+
+        make_identity(nc, ident_f[:])
+        load_scales(planes_w, W_scales)
+        make_identity(nc, ident_b[:])
+        for dst, src in (
+            (rk[0:3, H : 4 * H], W_gamma.partition_broadcast(3)),
+            (rk[3:6, H : 3 * H], U_gamma[0 : 2 * H].partition_broadcast(3)),
+            (rk[3:6, 0:H], U_gamma[2 * H : N3].partition_broadcast(3)),
+            (rk[6:7, H : 4 * H], W_beta.partition_broadcast(1)),
+            (rk[7:8, H : 4 * H], b.partition_broadcast(1)),
+            (rk[8:9, H : 3 * H], U_beta[0 : 2 * H].partition_broadcast(1)),
+            (rk[9:10, 0:H], U_beta[2 * H : N3].partition_broadcast(1)),
+        ):
+            nc.gpsimd.dma_start(out=dst, in_=src)
+        load_scales(planes_u, U_scales)
 
         def regroup(src, grp, first_bank):
             words = src[:].bitcast(F32)
@@ -173,8 +176,8 @@ def tile_lngrucell_w_kernel(
                         nc.vector.tensor_tensor(
                             out=prod[:, n0 : n0 + NB], in0=acc[:], in1=gam[:, n0 : n0 + NB], op=ALU.mult
                         )
-                if index in after:
-                    after[index]()
+                    for step in after.get(count, []):
+                        step()
             return late
 
         def finish(late, gam, prod):
@@ -207,10 +210,12 @@ def tile_lngrucell_w_kernel(
             nc.vector.tensor_tensor(out=rest[:], in0=shift[:], in1=c1, op=ALU.subtract)
             nc.vector.tensor_tensor(out=c2, in0=shift[:], in1=c1, op=ALU.subtract)
             nc.vector.tensor_tensor(out=c3, in0=rest[:], in1=c2, op=ALU.subtract)
-            ct = bank(ct_bank, [P, P], BF16)
-            nc.tensor.transpose(out=ct[:], in_=csp[:], identity=ident_b[:])
-            nc.scalar.copy(out=lhs[:], in_=ct[:])
-            return rstd, shift, lhs, diag
+            def fill_rows():
+                ct = bank(ct_bank, [P, P], BF16)
+                nc.tensor.transpose(out=ct[:], in_=csp[:], identity=ident_b[:])
+                nc.scalar.copy(out=lhs[:], in_=ct[:])
+
+            return rstd, shift, lhs, diag, fill_rows
 
         def cs(gate, j):
             return slice(gate * H + NB * j, gate * H + NB * (j + 1))
@@ -230,35 +235,42 @@ def tile_lngrucell_w_kernel(
         late_w = project(
             W_words, planes_w, cod_x, pln_x, g_w, p_w, st_w,
             [(0, H, 1), (H, H, 1), (2 * H, 1024, 2), (2 * H + 1024, NB, 4), (2 * H + 1536, NB, 4)],
-            {0: lambda: spread(g_u, 48, range(6, 9), False), 1: lambda: spread(g_u, 48, range(9, 12), False)},
+            {4: [lambda: spread(g_u, 48, range(6, 9), False)], 8: [lambda: spread(g_u, 48, range(9, 12), False)]},
         )
-        d1 = [None, None]
-        d0 = []
+        d1 = {}
+        d0 = {}
 
         def open_group(held, diag, gate, j, where):
-            d = bank(where, [P, NB], F32)
-            scale_pass(d, diag, p_w[:, cs(gate, j)], True)
-            held.append(d)
+            held[j] = bank(where, [P, NB], F32)
+            scale_pass(held[j], diag, p_w[:, cs(gate, j)], True)
 
-        def open_first(diag):
-            open_group(d1, diag, 1, 2, 4)
-            open_group(d1, diag, 1, 3, 5)
-
-        rstd_w, shift_w, lhs_w, diag_w = ln_scalars(st_w, 0, "w", late_w, g_w, p_w, 0, open_first)
-        open_group(d0, diag_w, 0, 0, 6)
-        open_group(d0, diag_w, 0, 1, 7)
+        rstd_w, shift_w, lhs_w, diag_w, fill_w = ln_scalars(st_w, 0, "w", late_w, g_w, p_w, 3, lambda diag: None)
         sw = rstd_w[:, 0:1]
-        for i, (col, dst) in enumerate(
-            [(3 * H + NB * j, cs(2, j)) for j in range(4)] + [(H, cs(1, 0)), (H + NB, cs(1, 1))]
-        ):
-            r_ps = bank((i + 1) % 3, [P, NB], F32)
+
+        def input_term(col, dst):
+            r_ps = bank(3, [P, NB], F32)
             rank_pass(r_ps, lhs_w, col, True)
             stt(p_w[:, dst], p_w[:, dst], sw, r_ps[:])
 
+        def candidate_term(j):
+            return lambda: input_term(3 * H + NB * j, cs(2, j))
+
+        def reset_term(j):
+            return lambda: input_term(2 * H + NB * j, cs(1, j))
+
         late_u = project(
             U_words, planes_u, cod_h, pln_h, g_u, p_u, st_u,
-            [(H, H, 1), (2 * H, H, 1), (0, 1024, 2), (1024, NB, 4), (1536, NB, 1)],
-            {},
+            [(H, 1024, 2), (H + 1024, 1024, 2), (2 * H, 1024, 2), (2 * H + 1024, 1024, 2), (0, 1024, 2)]
+            + [(2 * NB, NB, 4), (3 * NB, NB, 1)],
+            {
+                1: [fill_w, lambda: open_group(d1, diag_w, 1, 2, 4)],
+                2: [candidate_term(0), lambda: open_group(d1, diag_w, 1, 3, 5)],
+                3: [candidate_term(1), lambda: open_group(d0, diag_w, 0, 0, 6)],
+                4: [candidate_term(2), lambda: open_group(d0, diag_w, 0, 1, 7)],
+                5: [candidate_term(3)],
+                6: [reset_term(0)],
+                7: [reset_term(1)],
+            },
         )
 
         open_group(d0, diag_w, 0, 2, 0)
@@ -269,13 +281,14 @@ def tile_lngrucell_w_kernel(
             h2[j] = bank(where, [P, NB], F32)
             scale_pass(h2[j], diag, p_u[:, cs(2, j)], True)
 
-        rstd_u, shift_u, lhs_a, diag_u = ln_scalars(
+        rstd_u, shift_u, lhs_a, diag_u, fill_u = ln_scalars(
             st_u, 3, "u", late_u, g_u, p_u, 2, lambda diag: hidden_scale(0, 3, diag)
         )
+        fill_u()
         su = rstd_u[:, 0:1]
 
         def hidden_rank(j):
-            rank_pass(h2[j], lhs_a, 2 * H + NB * j, False)
+            rank_pass(h2[j], lhs_a, NB * j, False)
 
         def hidden(j, where):
             hidden_scale(j, where, diag_u)
@@ -295,7 +308,7 @@ def tile_lngrucell_w_kernel(
 
         def update(j):
             scale_pass(d0[j], diag_u, p_u[:, cs(0, j)], False)
-            rank_pass(d0[j], lhs_a, NB * j, False)
+            rank_pass(d0[j], lhs_a, H + NB * j, False)
             nc.scalar.activation(out=p_u[:, cs(0, j)], in_=d0[j][:], func=ACT.Sigmoid)
 
         def diff(j):
@@ -313,10 +326,10 @@ def tile_lngrucell_w_kernel(
         for j in range(2):
             stt(p_u[:, cs(1, j)], g_u[:, cs(1, j)], shift_u[:, 0:1], p_u[:, cs(1, j)])
             reset_gate(j)
-        rank_pass(d1[2], lhs_a, H + NB * 2, False)
+        rank_pass(d1[2], lhs_a, 2 * H + NB * 2, False)
         stt(p_u[:, cs(1, 2)], p_u[:, cs(1, 2)], su, d1[2][:])
         reset_gate(2)
-        rank_pass(d1[3], lhs_a, H + NB * 3, False)
+        rank_pass(d1[3], lhs_a, 2 * H + NB * 3, False)
         hidden_rank(0)
         gated(0)
         stt(p_u[:, cs(1, 3)], p_u[:, cs(1, 3)], su, d1[3][:])

@@ -26,7 +26,9 @@ def tile_lngrucell_w_kernel(
     nc = tc.nc
     with ExitStack() as ctx:
         keep = ctx.enter_context(tc.tile_pool(name="keep", bufs=1))
-        wpool = ctx.enter_context(tc.tile_pool(name="wpool", bufs=12))
+        wpool = ctx.enter_context(tc.tile_pool(name="wpool", bufs=5))
+        spool = ctx.enter_context(tc.tile_pool(name="spool", bufs=2))
+        lpool = ctx.enter_context(tc.tile_pool(name="lpool", bufs=4))
         psum = ctx.enter_context(tc.psum_pool(name="psum", bufs=1))
         ctx.enter_context(tc.manual_schedule())
 
@@ -148,9 +150,10 @@ def tile_lngrucell_w_kernel(
             for index, (c0, width, per) in enumerate(blocks):
                 tiles = []
                 for t in range(KG // per):
-                    wt = wpool.tile([P, H], I32, name="wt", tag="wt", align_bytes=64)
+                    pool = {4096: wpool, 2048: spool, 512: lpool}[per * width]
+                    wt = pool.tile([P, per * width], I32, name="wt", tag="wt", align_bytes=64)
                     nc.sync.dma_start(
-                        out=wt[:, 0 : per * width].rearrange("p (g n) -> p g n", g=per),
+                        out=wt[:].rearrange("p (g n) -> p g n", g=per),
                         in_=w32[:, t * per : (t + 1) * per, c0 : c0 + width],
                     )
                     tiles.append(wt)
@@ -234,7 +237,7 @@ def tile_lngrucell_w_kernel(
 
         late_w = project(
             W_words, planes_w, cod_x, pln_x, g_w, p_w, st_w,
-            [(0, H, 1), (H, H, 1), (2 * H, 1024, 2), (2 * H + 1024, NB, 4), (2 * H + 1536, NB, 4)],
+            [(0, H, 2), (H, H, 2), (2 * H, 1024, 4), (2 * H + 1024, NB, 4), (2 * H + 1536, NB, 4)],
             {4: [lambda: spread(g_u, 48, range(6, 9), False)], 8: [lambda: spread(g_u, 48, range(9, 12), False)]},
         )
         d1 = {}
@@ -260,7 +263,7 @@ def tile_lngrucell_w_kernel(
 
         late_u = project(
             U_words, planes_u, cod_h, pln_h, g_u, p_u, st_u,
-            [(H, 1024, 2), (H + 1024, 1024, 2), (2 * H, 1024, 2), (2 * H + 1024, 1024, 2), (0, 1024, 2)]
+            [(H, 1024, 4), (H + 1024, 1024, 4), (2 * H, 1024, 4), (2 * H + 1024, 1024, 4), (0, 1024, 4)]
             + [(2 * NB, NB, 4), (3 * NB, NB, 1)],
             {
                 1: [fill_w, lambda: open_group(d1, diag_w, 1, 2, 4)],

@@ -55,7 +55,8 @@ def tile_lngrucell_w_kernel(
         p_w = keep.tile([P, N3], F32, name="p_w")
         p_u = keep.tile([P, N3], F32, name="p_u")
         st_w = keep.tile([P, 12, 6], F32, name="st_w")
-        st_u = keep.tile([P, 12, 6], F32, name="st_u")
+        st_u = keep.tile([P, 8, 6], F32, name="st_u")
+        st_end = keep.tile([P, 27], F32, name="st_end")
         csp = keep.tile([P, P], BF16, name="csp")
         neghalf = keep.tile([P, 1], F32, name="neghalf")
         warm_in = keep.tile([P, 1], F32, name="warm_in")
@@ -66,6 +67,7 @@ def tile_lngrucell_w_kernel(
         nc.vector.memset(rk[:].bitcast(I32), 0)
         nc.vector.memset(warm_in[:], 0.0)
         nc.vector.memset(neghalf[:], -0.5)
+        nc.vector.memset(st_end[:, 0:1], 8.0 * NB)
         nc.vector.memset(csp[:], 0.0)
         nc.vector.memset(csp[:, 6:10], 1.0)
 
@@ -171,7 +173,7 @@ def tile_lngrucell_w_kernel(
                             start=(g == 0),
                             stop=(g == KG - 1),
                         )
-                    nc.vector.bn_stats(out=stats[:, count, :], in_=acc[:])
+                    nc.vector.bn_stats(out=stats(count), in_=acc[:])
                     count += 1
                     if count == 12:
                         late = (acc, n0)
@@ -236,7 +238,7 @@ def tile_lngrucell_w_kernel(
             nc.vector.tensor_tensor(out=dst, in0=in0, in1=in1, op=op)
 
         late_w = project(
-            W_words, planes_w, cod_x, pln_x, g_w, p_w, st_w,
+            W_words, planes_w, cod_x, pln_x, g_w, p_w, lambda k: st_w[:, k, :],
             [(0, H, 2), (H, H, 2), (2 * H, 1024, 4), (2 * H + 1024, NB, 4), (2 * H + 1536, NB, 4)],
             {4: [lambda: spread(g_u, 48, range(6, 9), False)], 8: [lambda: spread(g_u, 48, range(9, 12), False)]},
         )
@@ -261,8 +263,14 @@ def tile_lngrucell_w_kernel(
         def reset_term(j):
             return lambda: input_term(2 * H + NB * j, cs(1, j))
 
+        def sum_up():
+            nc.vector.bn_aggr(out=st_end[:, 1:3], in_=st_u[:].rearrange("p j s -> p (j s)"))
+            nc.vector.tensor_scalar(
+                out=st_end[:, 2:3], in0=st_end[:, 2:3], scalar1=8.0 * NB, scalar2=EPS * N3, op0=ALU.mult, op1=ALU.add
+            )
+
         late_u = project(
-            U_words, planes_u, cod_h, pln_h, g_u, p_u, st_u,
+            U_words, planes_u, cod_h, pln_h, g_u, p_u, lambda k: st_u[:, k, :] if k < 8 else st_end[:, 6 * k - 45 : 6 * k - 39],
             [(H, 1024, 4), (H + 1024, 1024, 4), (2 * H, 1024, 4), (2 * H + 1024, 1024, 4), (0, 1024, 4)]
             + [(2 * NB, NB, 4), (3 * NB, NB, 1)],
             {
@@ -273,6 +281,7 @@ def tile_lngrucell_w_kernel(
                 5: [candidate_term(3)],
                 6: [reset_term(0)],
                 7: [reset_term(1)],
+                8: [sum_up],
             },
         )
 
@@ -280,21 +289,33 @@ def tile_lngrucell_w_kernel(
         open_group(d0, diag_w, 0, 3, 1)
         h2 = [None] * 4
 
-        def hidden_scale(j, where, diag):
+        def hidden_scale(j, where):
             h2[j] = bank(where, [P, NB], F32)
-            scale_pass(h2[j], diag, p_u[:, cs(2, j)], True)
+            scale_pass(h2[j], diag_u, p_u[:, cs(2, j)], True)
 
-        rstd_u, shift_u, lhs_a, diag_u, fill_u = ln_scalars(
-            st_u, 3, "u", late_u, g_u, p_u, 2, lambda diag: hidden_scale(0, 3, diag)
-        )
-        fill_u()
+        mv_u = keep.tile([P, 2], F32, name="mv_u")
+        rstd_u = keep.tile([P, 1], F32, name="rstd_u")
+        shift_u = keep.tile([P, 1], F32, name="shift_u")
+        rest_u = keep.tile([P, 1], F32, name="rest_u")
+        lhs_a = keep.tile([P, P], BF16, name="lhs_a")
+        diag_u = keep.tile([P, P], F32, name="diag_u")
+        mean_u = mv_u[:, 0:1]
         su = rstd_u[:, 0:1]
+        c1, c2, c3 = (csp[:, 3 + i : 4 + i] for i in range(3))
+
+        def shift_into(dst):
+            nc.vector.tensor_scalar(out=dst, in0=mean_u, scalar1=su, scalar2=-1.0, op0=ALU.mult, op1=ALU.mult)
+
+        nc.vector.bn_aggr(out=mv_u[:], in_=st_end[:])
+        nc.gpsimd.tensor_tensor(out=rstd_u[:], in0=mv_u[:, 1:2], in1=neghalf[:], op=ALU.pow)
+        finish(late_u, g_u, p_u)
+        nc.scalar.activation(out=diag_u[:], in_=ident_f[:], func=ACT.Copy, scale=su)
 
         def hidden_rank(j):
             rank_pass(h2[j], lhs_a, NB * j, False)
 
         def hidden(j, where):
-            hidden_scale(j, where, diag_u)
+            hidden_scale(j, where)
             hidden_rank(j)
 
         def reset_gate(j):
@@ -309,8 +330,10 @@ def tile_lngrucell_w_kernel(
         def cand(j):
             nc.scalar.activation(out=p_u[:, cs(2, j)], in_=p_u[:, cs(2, j)], func=ACT.Tanh)
 
-        def update(j):
+        def update_scale(j):
             scale_pass(d0[j], diag_u, p_u[:, cs(0, j)], False)
+
+        def update(j):
             rank_pass(d0[j], lhs_a, H + NB * j, False)
             nc.scalar.activation(out=p_u[:, cs(0, j)], in_=d0[j][:], func=ACT.Sigmoid)
 
@@ -320,12 +343,24 @@ def tile_lngrucell_w_kernel(
         def weigh(j):
             tt(p_w[:, cs(0, j)], p_w[:, cs(0, j)], p_u[:, cs(0, j)], ALU.mult)
 
-        def blend(j):
-            tt(p_w[:, cs(0, j)], p_w[:, cs(0, j)], p_u[:, cs(2, j)], ALU.add)
-            nc.sync.dma_start(out=out[:, cs(0, j)], in_=p_w[:, cs(0, j)])
+        def blend(j, parts=1):
+            step = NB // parts
+            for k in range(parts):
+                piece = slice(NB * j + step * k, NB * j + step * (k + 1))
+                tt(p_w[:, piece], p_w[:, piece], p_u[:, 2 * H + NB * j + step * k : 2 * H + NB * j + step * (k + 1)], ALU.add)
+                nc.sync.dma_start(out=out[:, piece], in_=p_w[:, piece])
 
-        for j in range(2):
-            stt(p_u[:, cs(1, j)], p_u[:, cs(1, j)], su, p_w[:, cs(1, j)])
+        hidden_scale(0, 3)
+        shift_into(c1)
+        shift_into(shift_u[:])
+        tt(rest_u[:], shift_u[:], c1, ALU.subtract)
+        tt(c2, shift_u[:], c1, ALU.subtract)
+        stt(p_u[:, cs(1, 0)], p_u[:, cs(1, 0)], su, p_w[:, cs(1, 0)])
+        tt(c3, rest_u[:], c2, ALU.subtract)
+        stt(p_u[:, cs(1, 1)], p_u[:, cs(1, 1)], su, p_w[:, cs(1, 1)])
+        ct = bank(2, [P, P], BF16)
+        nc.tensor.transpose(out=ct[:], in_=csp[:], identity=ident_b[:])
+        nc.scalar.copy(out=lhs_a[:], in_=ct[:])
         for j in range(2):
             stt(p_u[:, cs(1, j)], g_u[:, cs(1, j)], shift_u[:, 0:1], p_u[:, cs(1, j)])
             reset_gate(j)
@@ -341,6 +376,7 @@ def tile_lngrucell_w_kernel(
         cand(0)
         hidden(1, 2)
         gated(1)
+        update_scale(0)
         cand_arg(1)
         update(0)
         cand(1)
@@ -350,6 +386,7 @@ def tile_lngrucell_w_kernel(
         weigh(0)
         cand_arg(2)
         blend(0)
+        update_scale(1)
         update(1)
         cand(2)
         diff(1)
@@ -358,12 +395,14 @@ def tile_lngrucell_w_kernel(
         weigh(1)
         cand_arg(3)
         blend(1)
+        update_scale(2)
         update(2)
         cand(3)
+        update_scale(3)
         update(3)
         diff(2)
         diff(3)
         weigh(2)
         weigh(3)
         blend(2)
-        blend(3)
+        blend(3, 2)

@@ -61,11 +61,13 @@ def tile_lngrucell_w_kernel(
         neghalf = keep.tile([P, 1], F32, name="neghalf")
         warm_in = keep.tile([P, 1], F32, name="warm_in")
         warm_out = keep.tile([P, 1], F32, name="warm_out")
+        warm_one = keep.tile([P, 1], F32, name="warm_one")
 
         nc.vector.memset(planes_w[:].bitcast(I32), 0)
         nc.vector.memset(planes_u[:].bitcast(I32), 0)
         nc.vector.memset(rk[:].bitcast(I32), 0)
         nc.vector.memset(warm_in[:], 0.0)
+        nc.vector.memset(warm_one[:], 1.0)
         nc.vector.memset(neghalf[:], -0.5)
         nc.vector.memset(st_end[:, 0:1], 8.0 * NB)
         nc.vector.memset(csp[:], 0.0)
@@ -282,6 +284,7 @@ def tile_lngrucell_w_kernel(
                 6: [reset_term(0)],
                 7: [reset_term(1)],
                 8: [sum_up],
+                10: [lambda: nc.scalar.activation(out=warm_out[:], in_=warm_one[:], func=ACT.Abs_reciprocal_sqrt)],
             },
         )
 
@@ -307,9 +310,10 @@ def tile_lngrucell_w_kernel(
             nc.vector.tensor_scalar(out=dst, in0=mean_u, scalar1=su, scalar2=-1.0, op0=ALU.mult, op1=ALU.mult)
 
         nc.vector.bn_aggr(out=mv_u[:], in_=st_end[:])
-        nc.gpsimd.tensor_tensor(out=rstd_u[:], in0=mv_u[:, 1:2], in1=neghalf[:], op=ALU.pow)
+        nc.scalar.activation(out=rstd_u[:], in_=mv_u[:, 1:2], func=ACT.Abs_reciprocal_sqrt)
         finish(late_u, g_u, p_u)
         nc.scalar.activation(out=diag_u[:], in_=ident_f[:], func=ACT.Copy, scale=su)
+        nc.scalar.activation(out=warm_out[:], in_=warm_in[:], func=ACT.Sigmoid)
 
         def hidden_rank(j):
             rank_pass(h2[j], lhs_a, NB * j, False)

@@ -63,6 +63,7 @@ def tile_lngrucell_w_kernel(
         warm_out = keep.tile([P, 1], F32, name="warm_out")
         warm_one = keep.tile([P, 1], F32, name="warm_one")
 
+        nc.vector.memset(vecrows[96:128, :], 0.0)
         nc.vector.memset(planes_w[:].bitcast(I32), 0)
         nc.vector.memset(planes_u[:].bitcast(I32), 0)
         nc.vector.memset(rk[:].bitcast(I32), 0)
@@ -74,10 +75,11 @@ def tile_lngrucell_w_kernel(
         nc.vector.memset(csp[:, 6:10], 1.0)
 
         nc.sync.dma_start(out=x_sb[:], in_=x_in)
-        nc.sync.dma_start(out=h_sb[:], in_=hx)
-        nc.scalar.dma_start(out=vecrows[0:48, :], in_=W_gamma.rearrange("(j p) -> j p", p=P))
-        nc.scalar.dma_start(out=vecrows[48:96, :], in_=U_gamma.rearrange("(j p) -> j p", p=P))
-        nc.scalar.dma_start(out=vecrows[96:128, :], in_=W_beta[0:4096].rearrange("(j p) -> j p", p=P))
+        nc.scalar.dma_start(out=h_sb[:], in_=hx)
+        for first, gamma in ((0, W_gamma), (48, U_gamma)):
+            rows = gamma.rearrange("(j p) -> j p", p=P)
+            nc.sync.dma_start(out=vecrows[first : first + 32, :], in_=rows[0:32, :])
+            nc.sync.dma_start(out=vecrows[first + 32 : first + 48, :], in_=rows[32:48, :])
         nc.scalar.activation(out=warm_out[:], in_=warm_in[:], func=ACT.Sigmoid)
 
         def load_scales(planes, scales):

from contextlib import ExitStack

import concourse.mybir as mybir
from concourse.masks import make_identity

F32 = mybir.dt.float32
BF16 = mybir.dt.bfloat16
I32 = mybir.dt.int32
U8 = mybir.dt.uint8
FP8X4 = mybir.dt.float8_e4m3fn_x4
ALU = mybir.AluOpType
ACT = mybir.ActivationFunctionType

P = 128
H = 2048
N3 = 3 * H
KG = 4
NB = 512
EPS = 1e-5
FLOPS = 2 * 2 * P * H * N3


def tile_lngrucell_w_kernel(
    tc, x_in, hx, W_words, W_scales, U_words, U_scales, b, W_gamma, W_beta, U_gamma, U_beta, out
):
    nc = tc.nc
    with ExitStack() as ctx:
        keep = ctx.enter_context(tc.tile_pool(name="keep", bufs=1))
        wpool = ctx.enter_context(tc.tile_pool(name="wpool", bufs=5))
        spool = ctx.enter_context(tc.tile_pool(name="spool", bufs=2))
        lpool = ctx.enter_context(tc.tile_pool(name="lpool", bufs=4))
        psum = ctx.enter_context(tc.psum_pool(name="psum", bufs=1))
        ctx.enter_context(tc.manual_schedule())

        def bank(i, shape, dtype):
            return psum.tile(shape, dtype, name="ps%d" % i, tag="b%d" % i)

        planes_w = keep.tile([P, N3], U8, name="planes_w", align_bytes=64)
        planes_u = keep.tile([P, N3], U8, name="planes_u", align_bytes=64)
        x_sb = keep.tile([P, H], BF16, name="x_sb", align_bytes=64)
        h_sb = keep.tile([P, H], BF16, name="h_sb", align_bytes=64)
        grp_x = keep.tile([P, H], BF16, name="grp_x", align_bytes=64)
        grp_h = keep.tile([P, H], BF16, name="grp_h", align_bytes=64)
        cod_x = keep.tile([P, H // 4], I32, name="cod_x", align_bytes=64)
        cod_h = keep.tile([P, H // 4], I32, name="cod_h", align_bytes=64)
        pln_x = keep.tile([P, H // 4], U8, name="pln_x", align_bytes=64)
        pln_h = keep.tile([P, H // 4], U8, name="pln_h", align_bytes=64)
        ident_f = keep.tile([P, P], F32, name="ident_f")
        ident_b = keep.tile([P, P], BF16, name="ident_b")
        vecrows = keep.tile([P, P], BF16, name="vecrows")
        g_t = keep.tile([P, P], BF16, name="g_t")
        g_w = keep.tile([P, N3], BF16, name="g_w")
        g_u = keep.tile([P, N3], BF16, name="g_u")
        rk = keep.tile([P, 4 * H], BF16, name="rk")
        p_w = keep.tile([P, N3], F32, name="p_w")
        p_u = keep.tile([P, N3], F32, name="p_u")
        st_w = keep.tile([P, 12, 6], F32, name="st_w")
        st_u = keep.tile([P, 8, 6], F32, name="st_u")
        st_end = keep.tile([P, 27], F32, name="st_end")
        csp = keep.tile([P, P], BF16, name="csp")
        neghalf = keep.tile([P, 1], F32, name="neghalf")
        warm_in = keep.tile([P, 1], F32, name="warm_in")
        warm_out = keep.tile([P, 1], F32, name="warm_out")
        warm_one = keep.tile([P, 1], F32, name="warm_one")

        nc.vector.memset(vecrows[96:128, :], 0.0)
        nc.vector.memset(planes_w[:].bitcast(I32), 0)
        nc.vector.memset(planes_u[:].bitcast(I32), 0)
        nc.vector.memset(rk[:].bitcast(I32), 0)
        nc.vector.memset(warm_in[:], 0.0)
        nc.vector.memset(warm_one[:], 1.0)
        nc.vector.memset(neghalf[:], -0.5)
        nc.vector.memset(st_end[:, 0:1], 8.0 * NB)
        nc.vector.memset(csp[:], 0.0)
        nc.vector.memset(csp[:, 6:10], 1.0)

        nc.sync.dma_start(out=x_sb[:], in_=x_in)
        nc.scalar.dma_start(out=h_sb[:], in_=hx)
        for first, gamma in ((0, W_gamma), (48, U_gamma)):
            rows = gamma.rearrange("(j p) -> j p", p=P)
            nc.sync.dma_start(out=vecrows[first : first + 32, :], in_=rows[0:32, :])
            nc.sync.dma_start(out=vecrows[first + 32 : first + 48, :], in_=rows[32:48, :])
        nc.scalar.activation(out=warm_out[:], in_=warm_in[:], func=ACT.Sigmoid)

        def load_scales(planes, scales):
            for q in range(4):
                nc.gpsimd.dma_start(
                    out=planes[32 * q : 32 * q + 16, :].bitcast(F32),
                    in_=scales.bitcast(F32)[:, 4 * q : 4 * q + 4, :],
                )

        make_identity(nc, ident_f[:])
        load_scales(planes_w, W_scales)
        make_identity(nc, ident_b[:])
        for dst, src in (
            (rk[0:3, H : 4 * H], W_gamma.partition_broadcast(3)),
            (rk[3:6, H : 3 * H], U_gamma[0 : 2 * H].partition_broadcast(3)),
            (rk[3:6, 0:H], U_gamma[2 * H : N3].partition_broadcast(3)),
            (rk[6:7, H : 4 * H], W_beta.partition_broadcast(1)),
            (rk[7:8, H : 4 * H], b.partition_broadcast(1)),
            (rk[8:9, H : 3 * H], U_beta[0 : 2 * H].partition_broadcast(1)),
            (rk[9:10, 0:H], U_beta[2 * H : N3].partition_broadcast(1)),
        ):
            nc.gpsimd.dma_start(out=dst, in_=src)
        load_scales(planes_u, U_scales)

        def regroup(src, grp, first_bank):
            words = src[:].bitcast(F32)
            gview = grp[:].bitcast(F32).rearrange("p (g r u) -> p g r u", g=KG, r=P, u=2)
            for half in range(2):
                xt = bank(first_bank + half, [P, 4, P], F32)
                for gg in range(2):
                    g = 2 * half + gg
                    for u in range(2):
                        nc.tensor.transpose(
                            out=xt[:, 2 * gg + u, :],
                            in_=words[:, 256 * g + u : 256 * (g + 1) : 2],
                            identity=ident_f[:],
                        )
                nc.vector.tensor_copy(
                    out=gview[:, 2 * half : 2 * half + 2, :, :],
                    in_=xt[:].rearrange("p (g u) r -> p g r u", g=2, u=2),
                )

        regroup(x_sb, grp_x, 0)
        nc.vector.quantize_mx(out=cod_x[:].bitcast(FP8X4), scales=pln_x[:], in_=grp_x[:])

        gt_ps = bank(2, [P, P], BF16)
        nc.tensor.transpose(out=gt_ps[:], in_=vecrows[:], identity=ident_b[:])
        nc.scalar.copy(out=g_t[:], in_=gt_ps[:])

        def spread(dst, first, blocks, share):
            for blk in blocks:
                pg = bank(3 + blk % 5, [P, NB], BF16)
                for i in range(4):
                    j = first + 4 * blk + i
                    nc.tensor.transpose(
                        out=pg[:, P * i : P * (i + 1)],
                        in_=g_t[:, j : j + 1].to_broadcast([P, P]),
                        identity=ident_b[:],
                    )
                if share and blk % 2 == 0:
                    nc.vector.tensor_copy(out=dst[:, NB * blk : NB * (blk + 1)], in_=pg[:])
                else:
                    nc.scalar.copy(out=dst[:, NB * blk : NB * (blk + 1)], in_=pg[:])

        spread(g_w, 0, range(12), True)
        regroup(h_sb, grp_h, 0)
        nc.vector.quantize_mx(out=cod_h[:].bitcast(FP8X4), scales=pln_h[:], in_=grp_h[:])
        spread(g_u, 48, range(0, 6), False)

        def project(words, planes, cod, pln, gam, prod, stats, blocks, after):
            w32 = words.rearrange("g p n t -> p g (n t)").bitcast(I32)
            count = 0
            late = None
            for index, (c0, width, per) in enumerate(blocks):
                tiles = []
                for t in range(KG // per):
                    pool = {4096: wpool, 2048: spool, 512: lpool}[per * width]
                    wt = pool.tile([P, per * width], I32, name="wt", tag="wt", align_bytes=64)
                    nc.sync.dma_start(
                        out=wt[:].rearrange("p (g n) -> p g n", g=per),
                        in_=w32[:, t * per : (t + 1) * per, c0 : c0 + width],
                    )
                    tiles.append(wt)
                for jj in range(width // NB):
                    n0 = c0 + NB * jj
                    acc = bank(count % 3, [P, NB], F32)
                    for g in range(KG):
                        lo = (g % per) * width + NB * jj
                        nc.tensor.matmul_mx(
                            out=acc[:],
                            lhsT=cod[:, P * g : P * (g + 1)].bitcast(FP8X4),
                            lhsT_scale=pln[:, P * g : P * (g + 1)],
                            rhs=tiles[g // per][:, lo : lo + NB].bitcast(FP8X4),
                            rhs_scale=planes[4 * g : P, n0 : n0 + NB],
                            start=(g == 0),
                            stop=(g == KG - 1),
                        )
                    nc.vector.bn_stats(out=stats(count), in_=acc[:])
                    count += 1
                    if count == 12:
                        late = (acc, n0)
                    else:
                        nc.vector.tensor_tensor(
                            out=prod[:, n0 : n0 + NB], in0=acc[:], in1=gam[:, n0 : n0 + NB], op=ALU.mult
                        )
                    for step in after.get(count, []):
                        step()
            return late

        def finish(late, gam, prod):
            acc, n0 = late
            nc.vector.tensor_tensor(out=prod[:, n0 : n0 + NB], in0=acc[:], in1=gam[:, n0 : n0 + NB], op=ALU.mult)

        def ln_scalars(stats, col, tagname, late, gam, prod, ct_bank, early):
            mv = keep.tile([P, 2], F32, name="mv_" + tagname)
            ve = keep.tile([P, 1], F32, name="ve_" + tagname)
            rstd = keep.tile([P, 1], F32, name="rstd_" + tagname)
            shift = keep.tile([P, 1], F32, name="shift_" + tagname)
            rest = keep.tile([P, 1], F32, name="rest_" + tagname)
            lhs = keep.tile([P, P], BF16, name="lhs_" + tagname)
            diag = keep.tile([P, P], F32, name="diag_" + tagname)
            nc.vector.bn_aggr(out=mv[:], in_=stats[:].rearrange("p j s -> p (j s)"))
            nc.vector.tensor_scalar_add(out=ve[:], in0=mv[:, 1:2], scalar1=EPS)
            nc.gpsimd.tensor_tensor(out=rstd[:], in0=ve[:], in1=neghalf[:], op=ALU.pow)
            finish(late, gam, prod)
            nc.scalar.activation(out=diag[:], in_=ident_f[:], func=ACT.Copy, scale=rstd[:, 0:1])
            early(diag)
            c1 = csp[:, col : col + 1]
            c2 = csp[:, col + 1 : col + 2]
            c3 = csp[:, col + 2 : col + 3]
            nc.vector.tensor_scalar(
                out=shift[:], in0=mv[:, 0:1], scalar1=rstd[:, 0:1], scalar2=-1.0, op0=ALU.mult, op1=ALU.mult
            )
            nc.vector.tensor_scalar(
                out=c1, in0=mv[:, 0:1], scalar1=rstd[:, 0:1], scalar2=-1.0, op0=ALU.mult, op1=ALU.mult
            )
            nc.vector.tensor_tensor(out=rest[:], in0=shift[:], in1=c1, op=ALU.subtract)
            nc.vector.tensor_tensor(out=c2, in0=shift[:], in1=c1, op=ALU.subtract)
            nc.vector.tensor_tensor(out=c3, in0=rest[:], in1=c2, op=ALU.subtract)
            def fill_rows():
                ct = bank(ct_bank, [P, P], BF16)
                nc.tensor.transpose(out=ct[:], in_=csp[:], identity=ident_b[:])
                nc.scalar.copy(out=lhs[:], in_=ct[:])

            return rstd, shift, lhs, diag, fill_rows

        def cs(gate, j):
            return slice(gate * H + NB * j, gate * H + NB * (j + 1))

        def rank_pass(dst, lhs, col, start):
            nc.tensor.matmul(out=dst[:], lhsT=lhs[:], rhs=rk[:, col : col + NB], start=start, stop=True)

        def scale_pass(dst, diag, src, start):
            nc.tensor.matmul(out=dst[:], lhsT=diag[:], rhs=src, start=start, stop=False)

        def stt(dst, in0, scalar, in1):
            nc.vector.scalar_tensor_tensor(out=dst, in0=in0, scalar=scalar, in1=in1, op0=ALU.mult, op1=ALU.add)

        def tt(dst, in0, in1, op):
            nc.vector.tensor_tensor(out=dst, in0=in0, in1=in1, op=op)

        late_w = project(
            W_words, planes_w, cod_x, pln_x, g_w, p_w, lambda k: st_w[:, k, :],
            [(0, H, 2), (H, H, 2), (2 * H, 1024, 4), (2 * H + 1024, NB, 4), (2 * H + 1536, NB, 4)],
            {4: [lambda: spread(g_u, 48, range(6, 9), False)], 8: [lambda: spread(g_u, 48, range(9, 12), False)]},
        )
        d1 = {}
        d0 = {}

        def open_group(held, diag, gate, j, where):
            held[j] = bank(where, [P, NB], F32)
            scale_pass(held[j], diag, p_w[:, cs(gate, j)], True)

        rstd_w, shift_w, lhs_w, diag_w, fill_w = ln_scalars(st_w, 0, "w", late_w, g_w, p_w, 3, lambda diag: None)
        sw = rstd_w[:, 0:1]

        def input_term(col, dst):
            r_ps = bank(3, [P, NB], F32)
            rank_pass(r_ps, lhs_w, col, True)
            stt(p_w[:, dst], p_w[:, dst], sw, r_ps[:])

        def candidate_term(j):
            return lambda: input_term(3 * H + NB * j, cs(2, j))

        def reset_term(j):
            return lambda: input_term(2 * H + NB * j, cs(1, j))

        def sum_up():
            nc.vector.bn_aggr(out=st_end[:, 1:3], in_=st_u[:].rearrange("p j s -> p (j s)"))
            nc.vector.tensor_scalar(
                out=st_end[:, 2:3], in0=st_end[:, 2:3], scalar1=8.0 * NB, scalar2=EPS * N3, op0=ALU.mult, op1=ALU.add
            )

        late_u = project(
            U_words, planes_u, cod_h, pln_h, g_u, p_u, lambda k: st_u[:, k, :] if k < 8 else st_end[:, 6 * k - 45 : 6 * k - 39],
            [(H, 1024, 4), (H + 1024, 1024, 4), (2 * H, 1024, 4), (2 * H + 1024, 1024, 4), (0, 1024, 4)]
            + [(2 * NB, NB, 4), (3 * NB, NB, 1)],
            {
                1: [fill_w, lambda: open_group(d1, diag_w, 1, 2, 4)],
                2: [candidate_term(0), lambda: open_group(d1, diag_w, 1, 3, 5)],
                3: [candidate_term(1), lambda: open_group(d0, diag_w, 0, 0, 6)],
                4: [candidate_term(2), lambda: open_group(d0, diag_w, 0, 1, 7)],
                5: [candidate_term(3)],
                6: [reset_term(0)],
                7: [reset_term(1)],
                8: [sum_up],
                10: [lambda: nc.scalar.activation(out=warm_out[:], in_=warm_one[:], func=ACT.Abs_reciprocal_sqrt)],
            },
        )

        open_group(d0, diag_w, 0, 2, 0)
        open_group(d0, diag_w, 0, 3, 1)
        h2 = [None] * 4

        def hidden_scale(j, where):
            h2[j] = bank(where, [P, NB], F32)
            scale_pass(h2[j], diag_u, p_u[:, cs(2, j)], True)

        mv_u = keep.tile([P, 2], F32, name="mv_u")
        rstd_u = keep.tile([P, 1], F32, name="rstd_u")
        shift_u = keep.tile([P, 1], F32, name="shift_u")
        rest_u = keep.tile([P, 1], F32, name="rest_u")
        lhs_a = keep.tile([P, P], BF16, name="lhs_a")
        diag_u = keep.tile([P, P], F32, name="diag_u")
        mean_u = mv_u[:, 0:1]
        su = rstd_u[:, 0:1]
        c1, c2, c3 = (csp[:, 3 + i : 4 + i] for i in range(3))

        def shift_into(dst):
            nc.vector.tensor_scalar(out=dst, in0=mean_u, scalar1=su, scalar2=-1.0, op0=ALU.mult, op1=ALU.mult)

        nc.vector.bn_aggr(out=mv_u[:], in_=st_end[:])
        nc.scalar.activation(out=rstd_u[:], in_=mv_u[:, 1:2], func=ACT.Abs_reciprocal_sqrt)
        finish(late_u, g_u, p_u)
        nc.scalar.activation(out=diag_u[:], in_=ident_f[:], func=ACT.Copy, scale=su)
        nc.scalar.activation(out=warm_out[:], in_=warm_in[:], func=ACT.Sigmoid)

        def hidden_rank(j):
            rank_pass(h2[j], lhs_a, NB * j, False)

        def hidden(j, where):
            hidden_scale(j, where)
            hidden_rank(j)

        def reset_gate(j):
            nc.scalar.activation(out=p_u[:, cs(1, j)], in_=p_u[:, cs(1, j)], func=ACT.Sigmoid)

        def gated(j):
            tt(p_u[:, cs(2, j)], p_u[:, cs(1, j)], h2[j][:], ALU.mult)

        def cand_arg(j):
            tt(p_u[:, cs(2, j)], p_u[:, cs(2, j)], p_w[:, cs(2, j)], ALU.add)

        def cand(j):
            nc.scalar.activation(out=p_u[:, cs(2, j)], in_=p_u[:, cs(2, j)], func=ACT.Tanh)

        def update_scale(j):
            scale_pass(d0[j], diag_u, p_u[:, cs(0, j)], False)

        def update(j):
            rank_pass(d0[j], lhs_a, H + NB * j, False)
            nc.scalar.activation(out=p_u[:, cs(0, j)], in_=d0[j][:], func=ACT.Sigmoid)

        def diff(j):
            tt(p_w[:, cs(0, j)], h_sb[:, cs(0, j)], p_u[:, cs(2, j)], ALU.subtract)

        def weigh(j):
            tt(p_w[:, cs(0, j)], p_w[:, cs(0, j)], p_u[:, cs(0, j)], ALU.mult)

        def blend(j, parts=1):
            step = NB // parts
            for k in range(parts):
                piece = slice(NB * j + step * k, NB * j + step * (k + 1))
                tt(p_w[:, piece], p_w[:, piece], p_u[:, 2 * H + NB * j + step * k : 2 * H + NB * j + step * (k + 1)], ALU.add)
                nc.sync.dma_start(out=out[:, piece], in_=p_w[:, piece])

        hidden_scale(0, 3)
        shift_into(c1)
        shift_into(shift_u[:])
        tt(rest_u[:], shift_u[:], c1, ALU.subtract)
        tt(c2, shift_u[:], c1, ALU.subtract)
        stt(p_u[:, cs(1, 0)], p_u[:, cs(1, 0)], su, p_w[:, cs(1, 0)])
        tt(c3, rest_u[:], c2, ALU.subtract)
        stt(p_u[:, cs(1, 1)], p_u[:, cs(1, 1)], su, p_w[:, cs(1, 1)])
        ct = bank(2, [P, P], BF16)
        nc.tensor.transpose(out=ct[:], in_=csp[:], identity=ident_b[:])
        nc.scalar.copy(out=lhs_a[:], in_=ct[:])
        for j in range(2):
            stt(p_u[:, cs(1, j)], g_u[:, cs(1, j)], shift_u[:, 0:1], p_u[:, cs(1, j)])
            reset_gate(j)
        rank_pass(d1[2], lhs_a, 2 * H + NB * 2, False)
        stt(p_u[:, cs(1, 2)], p_u[:, cs(1, 2)], su, d1[2][:])
        reset_gate(2)
        rank_pass(d1[3], lhs_a, 2 * H + NB * 3, False)
        hidden_rank(0)
        gated(0)
        stt(p_u[:, cs(1, 3)], p_u[:, cs(1, 3)], su, d1[3][:])
        reset_gate(3)
        cand_arg(0)
        cand(0)
        hidden(1, 2)
        gated(1)
        update_scale(0)
        cand_arg(1)
        update(0)
        cand(1)
        diff(0)
        hidden(2, 4)
        gated(2)
        weigh(0)
        cand_arg(2)
        blend(0)
        update_scale(1)
        update(1)
        cand(2)
        diff(1)
        hidden(3, 5)
        gated(3)
        weigh(1)
        cand_arg(3)
        blend(1)
        update_scale(2)
        update(2)
        cand(3)
        update_scale(3)
        update(3)
        diff(2)
        diff(3)
        weigh(2)
        weigh(3)
        blend(2)
        blend(3, 2)
